import numpy as np
import ml_dtypes


def mxq(x, axis, fmt="e4m3"):
    dtype, down = {"e4m3": (ml_dtypes.float8_e4m3fn, 7), "e5m2": (ml_dtypes.float8_e5m2, 14)}[fmt]
    v = np.moveaxis(np.asarray(x, np.float32).astype(ml_dtypes.bfloat16).astype(np.float64), axis, -1)
    blocks = v.reshape(v.shape[:-1] + (-1, 32))
    amax = np.abs(blocks).max(-1, keepdims=True)
    byte = np.maximum(np.where(amax > 0, np.frexp(amax)[1] - 1 + 127, 0) - down, 1)
    scale = np.exp2(byte - 127.0)
    codes = (blocks / scale).astype(np.float32).astype(dtype).astype(np.float64)
    return np.moveaxis((codes * scale).reshape(v.shape), -1, axis)


WIDE = False


def mx_kscale(k):
    if not WIDE:
        return np.ones(k)
    levels = np.array([10, -10, 5, -5, 0])
    a = np.random.permutation(np.resize(levels, k // 512 * 4)).reshape(k // 512, 4)
    idx = np.arange(k)
    return np.exp2(a[idx // 512, idx % 128 // 32])


BF16 = ml_dtypes.bfloat16


def bf(x):
    return np.asarray(x, np.float32).astype(BF16)


def f64(x):
    return np.asarray(x).astype(np.float64)


B, S, D = 32, 256, 512
NB = 2
W = 2 * NB + 1


def setup_inputs():
    s = mx_kscale(D)
    return {"x": bf(np.random.standard_normal((B, S, D)) * s),
            "Wq": bf(np.random.standard_normal((D, D)) / np.sqrt(D) / s[None, :]),
            "bq": bf(np.random.standard_normal(D) * 0.3),
            "k_proj": bf(np.random.standard_normal((B, S, D)))}


def reference(x, Wq, bq, k_proj):
    kf = f64(k_proj)
    q = (mxq(f64(x), 2, "e4m3") @ mxq(f64(Wq), 1, "e4m3").T) + f64(bq)
    scores = np.full((B, S, W), -np.inf)
    for j in range(W):
        o = j - NB
        lo, hi = max(0, -o), S - max(0, o)
        scores[:, lo:hi, j] = (q[:, lo:hi] * kf[:, lo + o:hi + o]).sum(-1) / np.sqrt(D)
    e = np.exp(scores - scores.max(-1, keepdims=True))
    return e / e.sum(-1, keepdims=True)

@@ -1,0 +1,215 @@
+import math
+from contextlib import ExitStack
+
+import concourse.bass as bass
+import concourse.mybir as mybir
+import concourse.tile as tile
+from concourse.masks import make_identity
+
+F32 = mybir.dt.float32
+BF16 = mybir.dt.bfloat16
+U32 = mybir.dt.uint32
+U8 = mybir.dt.uint8
+FP8X4 = mybir.dt.float8_e4m3fn_x4
+ALU = mybir.AluOpType
+ACT = mybir.ActivationFunctionType
+AX = mybir.AxisListType
+
+P = 128
+B, S, D = 32, 256, 512
+W = 5
+NB = 2
+R = 64
+QB = S // R
+HR = R + 2 * NB
+SCALE = 1.0 / math.sqrt(D)
+NEG = -1.0e30
+GROUP = 4
+G_TILES = frozenset(r for r in range(60) if r % 5 in (1, 3))
+SOFT_ENDS = (16, 32, 48, 60, 64)
+SOFT = 16
+
+FLOPS = 2 * B * S * D * D + 2 * B * S * W * D
+
+
+def tile_crosssliceattention_pa_t_kernel(tc, x, Wq, bq, k_proj, out):
+    nc = tc.nc
+    x_v = x.rearrange("b (q r) d -> (b q) r d", r=R)
+    k_v = k_proj.rearrange("b (q r) d -> (b q) r d", r=R)
+    k_h = k_proj.rearrange("b (q r) d -> b q r d", r=R)
+    out_v = out.rearrange("b (q r) j -> (b q) r j", r=R)
+
+    with ExitStack() as ctx:
+        keep = ctx.enter_context(tc.tile_pool(name="keep", bufs=1))
+        stage = ctx.enter_context(tc.tile_pool(name="stage", bufs=2))
+        small = ctx.enter_context(tc.tile_pool(name="small", bufs=2))
+        gpool = ctx.enter_context(tc.tile_pool(name="gpool", bufs=3))
+        ps_xt = ctx.enter_context(tc.psum_pool(name="ps_xt", bufs=2))
+        ps_q = ctx.enter_context(tc.psum_pool(name="ps_q", bufs=4))
+        ps_kt = ctx.enter_context(tc.psum_pool(name="ps_kt", bufs=1))
+        ps_c = ctx.enter_context(tc.psum_pool(name="ps_c", bufs=1))
+
+        ident = keep.tile([P, P], F32)
+        make_identity(nc, ident[:])
+
+        x_sb = keep.tile([P, R, D], BF16)
+        k_sb = keep.tile([P, HR, D], BF16)
+        w_sb = keep.tile([P, 4, D], BF16)
+        b_cols = keep.tile([P, 4], BF16)
+        w_codes = keep.tile([P, D], U32, align_bytes=64)
+        w_scales = keep.tile([P, D], U8, align_bytes=64)
+        sc = keep.tile([P, R, 8], F32)
+        c_sb = keep.tile([P, HR], F32)
+        out_sb = keep.tile([P, R, W], F32)
+        f_lo = keep.tile([P, 1], F32)
+        f_hi = keep.tile([P, 1], F32)
+
+        nc.vector.memset(k_sb[:, 0:NB, :], 0.0)
+        nc.vector.memset(k_sb[:, R + NB : HR, :], 0.0)
+        nc.sync.dma_start(out=w_sb[:], in_=Wq.rearrange("(c p) d -> p c d", p=P))
+        nc.sync.dma_start(out=x_sb[:, 0:4, :], in_=x_v[:, 0:4, :])
+        for q in range(1, QB):
+            nc.sync.dma_start(out=k_sb[q:P:QB, 0:NB, :], in_=k_h[:, q - 1, R - NB : R, :])
+        nc.sync.dma_start(out=k_sb[:, NB : NB + 8, :], in_=k_v[:, 0:8, :])
+        nc.sync.dma_start(out=x_sb[:, 4:8, :], in_=x_v[:, 4:8, :])
+        for g in range(1, 8):
+            nc.sync.dma_start(out=k_sb[:, NB + 8 * g : NB + 8 * g + 8, :], in_=k_v[:, 8 * g : 8 * g + 8, :])
+            nc.sync.dma_start(out=x_sb[:, 8 * g : 8 * g + 8, :], in_=x_v[:, 8 * g : 8 * g + 8, :])
+        for q in range(0, QB - 1):
+            nc.sync.dma_start(out=k_sb[q:P:QB, R + NB : HR, :], in_=k_h[:, q + 1, 0:NB, :])
+        with nc.allow_non_contiguous_dma(reason="bias, two neighbouring values to a partition"):
+            nc.scalar.dma_start(
+                out=b_cols[:].rearrange("w (u e) -> w u e", e=2),
+                in_=bq.rearrange("(u w e) -> w u e", u=2, e=2),
+            )
+
+        nc.vector.tensor_reduce(out=f_lo[:], in_=ident[:, 0:P:QB], axis=AX.X, op=ALU.add)
+        nc.vector.tensor_reduce(out=f_hi[:], in_=ident[:, QB - 1 : P : QB], axis=AX.X, op=ALU.add)
+        nc.vector.tensor_scalar_mul(out=f_lo[:], in0=f_lo[:], scalar1=NEG)
+        nc.vector.tensor_scalar_mul(out=f_hi[:], in0=f_hi[:], scalar1=NEG)
+
+        def quantise_four(words_of, codes, scales):
+            grouped = stage.tile([P, GROUP * P, 4], BF16, align_bytes=64, tag="grouped")
+            g32 = grouped[:].bitcast(F32)
+            for h in range(2):
+                xt = ps_xt.tile([P, 2, 2, P], F32, tag="xt")
+                for i in range(2):
+                    for u in range(2):
+                        nc.tensor.transpose(xt[:, i, u, :], words_of(2 * h + i)[:, u * P : (u + 1) * P], ident[:])
+                nc.scalar.copy(
+                    out=g32[:, 2 * h * P : (2 * h + 2) * P, :].rearrange("p (i t) u -> p i t u", i=2),
+                    in_=xt[:].rearrange("p i u t -> p i t u"),
+                )
+            nc.vector.quantize_mx(
+                out=codes.bitcast(FP8X4),
+                scales=scales,
+                in_=grouped[:].rearrange("p t j -> p (t j)"),
+            )
+
+        w32 = w_sb[:].bitcast(F32)
+        x32 = x_sb[:].bitcast(F32)
+        k32 = k_sb[:].bitcast(F32)
+        quantise_four(lambda i: w32[:, i, :], w_codes[:], w_scales[:])
+
+        c_ps = ps_c.tile([P, HR], F32)
+
+        def bias_dot(i0):
+            kt = ps_kt.tile([P, 2, 2, P], F32, tag="kt")
+            for i in range(2):
+                for u in range(2):
+                    nc.tensor.transpose(kt[:, i, u, :], k32[:, i0 + i, u * P : (u + 1) * P], ident[:])
+            kt_sb = stage.tile([P, 2, 2, P], F32, tag="kt_sb")
+            nc.scalar.copy(out=kt_sb[:], in_=kt[:])
+            kt_bf = kt_sb[:].bitcast(BF16).rearrange("p i u (t e) -> p i u t e", e=2)
+            for i in range(2):
+                for n in range(4):
+                    nc.tensor.matmul(
+                        out=c_ps[:, i0 + i : i0 + i + 1],
+                        lhsT=kt_bf[:, i, n // 2, :, n % 2],
+                        rhs=b_cols[:, n : n + 1],
+                        start=(n == 0),
+                        stop=(n == 3),
+                    )
+
+        def softmax(r0, r1):
+            n = r1 - r0
+            t1 = small.tile([P, SOFT, W], F32, tag="t1")
+            for j in range(W):
+                nc.vector.tensor_tensor(
+                    out=t1[:, 0:n, j], in0=sc[:, r0:r1, j], in1=c_sb[:, r0 + j : r1 + j], op=ALU.add
+                )
+            for r, j0, j1, flag in ((0, 0, 2, f_lo), (1, 0, 1, f_lo), (R - 2, 4, 5, f_hi), (R - 1, 3, 5, f_hi)):
+                if r0 <= r < r1:
+                    nc.vector.tensor_scalar_add(
+                        out=t1[:, r - r0, j0:j1], in0=t1[:, r - r0, j0:j1], scalar1=flag[:, 0:1]
+                    )
+            mx = small.tile([P, SOFT], F32, tag="mx")
+            nc.vector.tensor_reduce(out=mx[:, 0:n], in_=t1[:, 0:n, :], axis=AX.X, op=ALU.max)
+            nc.vector.tensor_tensor(
+                out=t1[:, 0:n, :], in0=t1[:, 0:n, :], in1=mx[:, 0:n].unsqueeze(2).to_broadcast([P, n, W]), op=ALU.subtract
+            )
+            ex = small.tile([P, SOFT, W], F32, tag="ex")
+            nc.scalar.activation(out=ex[:, 0:n, :], in_=t1[:, 0:n, :], func=ACT.Exp)
+            sm = small.tile([P, SOFT], F32, tag="sm")
+            nc.vector.tensor_reduce(out=sm[:, 0:n], in_=ex[:, 0:n, :], axis=AX.X, op=ALU.add)
+            nc.vector.reciprocal(out=sm[:, 0:n], in_=sm[:, 0:n])
+            nc.vector.tensor_tensor(
+                out=out_sb[:, r0:r1, :], in0=ex[:, 0:n, :], in1=sm[:, 0:n].unsqueeze(2).to_broadcast([P, n, W]), op=ALU.mult
+            )
+            nc.sync.dma_start(out=out_v[:, r0:r1, :], in_=out_sb[:, r0:r1, :])
+
+        next_c = 0
+        c_copied = 0
+        soft_done = 0
+        for g in range(R // GROUP):
+            x_codes = stage.tile([P, GROUP * P], U32, align_bytes=64, tag="x_codes")
+            x_scales = stage.tile([P, GROUP * P], U8, align_bytes=64, tag="x_scales")
+            quantise_four(lambda i: x32[:, GROUP * g + i, :], x_codes[:], x_scales[:])
+            while next_c < min(HR, GROUP * g + 8):
+                bias_dot(next_c)
+                next_c += 2
+            for i in range(GROUP):
+                r = GROUP * g + i
+                q0 = ps_q.tile([P, D], F32, tag="q0")
+                nc.tensor.matmul_mx(
+                    out=q0[:],
+                    lhsT=x_codes[:, i * P : (i + 1) * P].bitcast(FP8X4),
+                    lhsT_scale=x_scales[:, i * P : (i + 1) * P],
+                    rhs=w_codes[:].bitcast(FP8X4),
+                    rhs_scale=w_scales[:],
+                    start=True,
+                    stop=True,
+                )
+                if r in G_TILES:
+                    q_sb = gpool.tile([P, D], F32, tag="q_sb")
+                    nc.scalar.mul(out=q_sb[:], in_=q0[:], mul=SCALE)
+                    prod = gpool.tile([P, W, D], F32, tag="prod")
+                    nc.gpsimd.tensor_tensor(
+                        out=prod[:],
+                        in0=q_sb[:].unsqueeze(1).to_broadcast([P, W, D]),
+                        in1=k_sb[:, r : r + W, :],
+                        op=ALU.mult,
+                    )
+                    for j in range(W):
+                        s_junk = stage.tile([P, D], BF16, tag="s_junk")
+                        nc.scalar.activation(
+                            out=s_junk[:], in_=prod[:, j, :], func=ACT.Copy, accum_out=sc[:, r, j : j + 1]
+                        )
+                else:
+                    for j in range(W):
+                        v_junk = stage.tile([P, D], F32, tag="v_junk")
+                        nc.vector.scalar_tensor_tensor(
+                            out=v_junk[:],
+                            in0=q0[:],
+                            scalar=SCALE,
+                            in1=k_sb[:, r + j, :],
+                            op0=ALU.mult,
+                            op1=ALU.mult,
+                            accum_out=sc[:, r, j : j + 1],
+                        )
+            done = GROUP * (g + 1)
+            if done in SOFT_ENDS:
+                nc.scalar.mul(out=c_sb[:, c_copied : done + 4], in_=c_ps[:, c_copied : done + 4], mul=SCALE)
+                c_copied = done + 4
+                softmax(soft_done, done)
+                soft_done = done

@@ -1,9 +1,7 @@
 import math
 from contextlib import ExitStack
 
-import concourse.bass as bass
 import concourse.mybir as mybir
-import concourse.tile as tile
 from concourse.masks import make_identity
 
 F32 = mybir.dt.float32
@@ -24,12 +22,62 @@ QB = S // R
 HR = R + 2 * NB
 SCALE = 1.0 / math.sqrt(D)
 NEG = -1.0e30
-GROUP = 4
-G_TILES = frozenset(r for r in range(60) if r % 5 in (1, 3))
-SOFT_ENDS = (16, 32, 48, 60, 64)
-SOFT = 16
+NG = 24
+NV = R - NG
+V_CHUNKS = ((0, 16), (16, 32), (32, NV - 2), (NV - 2, NV))
+G_CHUNKS = ((52, 64), (NV + 3, 52), (NV, NV + 3))
+
+T_V = 2.35
+T_G = 4.45
+LOG = []
 
 FLOPS = 2 * B * S * D * D + 2 * B * S * W * D
+
+
+def run_schedule(tasks, slots):
+    n = len(tasks)
+    fin = [-1.0] * n
+    busy = {"T": 0.0, "S": 0.0, "V": 0.0, "G": 0.0, "D": 0.0}
+    todo = list(range(n))
+    while todo:
+        best = None
+        for i in todo:
+            eng, dur, deps, emit, due, take, give = tasks[i]
+            est = busy.get(eng, 0.0)
+            ok = True
+            for d in deps:
+                if fin[d] < 0.0:
+                    ok = False
+                    break
+                est = max(est, fin[d])
+            if not ok:
+                continue
+            if take is not None:
+                free = [f for f in slots[take[0]] if f >= 0.0]
+                if not free:
+                    continue
+                est = max(est, min(free))
+            key = (est, due, i)
+            if best is None or key < best:
+                best = key
+        assert best is not None
+        est, due, i = best
+        eng, dur, deps, emit, due, take, give = tasks[i]
+        if take is not None:
+            pool = slots[take[0]]
+            free = min(f for f in pool if f >= 0.0)
+            k = pool.index(free)
+            pool[k] = -1.0
+            take[1][take[0]] = k
+        fin[i] = est + dur
+        if eng in busy:
+            busy[eng] = fin[i]
+        if give is not None:
+            slots[give[0]][give[1][give[0]]] = fin[i]
+        if emit is not None:
+            emit()
+        LOG.append((eng, est, fin[i], i))
+        todo = [j for j in todo if j != i]
 
 
 def tile_crosssliceattention_pa_t_kernel(tc, x, Wq, bq, k_proj, out):
@@ -41,175 +89,325 @@ def tile_crosssliceattention_pa_t_kernel(tc, x, Wq, bq, k_proj, out):
 
     with ExitStack() as ctx:
         keep = ctx.enter_context(tc.tile_pool(name="keep", bufs=1))
-        stage = ctx.enter_context(tc.tile_pool(name="stage", bufs=2))
-        small = ctx.enter_context(tc.tile_pool(name="small", bufs=2))
-        gpool = ctx.enter_context(tc.tile_pool(name="gpool", bufs=3))
-        ps_xt = ctx.enter_context(tc.psum_pool(name="ps_xt", bufs=2))
-        ps_q = ctx.enter_context(tc.psum_pool(name="ps_q", bufs=4))
-        ps_kt = ctx.enter_context(tc.psum_pool(name="ps_kt", bufs=1))
-        ps_c = ctx.enter_context(tc.psum_pool(name="ps_c", bufs=1))
+        psum = ctx.enter_context(tc.psum_pool(name="psum", bufs=1))
+        ctx.enter_context(tc.manual_schedule())
 
-        ident = keep.tile([P, P], F32)
-        make_identity(nc, ident[:])
+        ident = keep.tile([P, P], F32, name="ident")
+        x_sb = keep.tile([P, R, D], BF16, name="x_sb")
+        k_sb = keep.tile([P, HR, D], BF16, name="k_sb")
+        w_sb = keep.tile([P, 4, D], BF16, name="w_sb")
+        b_cols = keep.tile([P, 4], BF16, name="b_cols")
+        w_codes = keep.tile([P, D], U32, align_bytes=64, name="w_codes")
+        w_scales = keep.tile([P, D], U8, align_bytes=64, name="w_scales")
+        sc = keep.tile([P, R, 8], F32, name="sc")
+        c_sb = keep.tile([P, HR], F32, name="c_sb")
+        out_sb = keep.tile([P, R, W], F32, name="out_sb")
+        f_lo = keep.tile([P, 1], F32, name="f_lo")
+        f_hi = keep.tile([P, 1], F32, name="f_hi")
+        v_junk = keep.tile([P, D], F32, name="v_junk")
+        s_junk = keep.tile([P, D], BF16, name="s_junk")
+        banks = [psum.tile([P, 512], F32, name="bank%d" % i) for i in range(8)]
+        c_ps = banks[7]
 
-        x_sb = keep.tile([P, R, D], BF16)
-        k_sb = keep.tile([P, HR, D], BF16)
-        w_sb = keep.tile([P, 4, D], BF16)
-        b_cols = keep.tile([P, 4], BF16)
-        w_codes = keep.tile([P, D], U32, align_bytes=64)
-        w_scales = keep.tile([P, D], U8, align_bytes=64)
-        sc = keep.tile([P, R, 8], F32)
-        c_sb = keep.tile([P, HR], F32)
-        out_sb = keep.tile([P, R, W], F32)
-        f_lo = keep.tile([P, 1], F32)
-        f_hi = keep.tile([P, 1], F32)
-
-        nc.vector.memset(k_sb[:, 0:NB, :], 0.0)
-        nc.vector.memset(k_sb[:, R + NB : HR, :], 0.0)
-        nc.sync.dma_start(out=w_sb[:], in_=Wq.rearrange("(c p) d -> p c d", p=P))
-        nc.sync.dma_start(out=x_sb[:, 0:4, :], in_=x_v[:, 0:4, :])
-        for q in range(1, QB):
-            nc.sync.dma_start(out=k_sb[q:P:QB, 0:NB, :], in_=k_h[:, q - 1, R - NB : R, :])
-        nc.sync.dma_start(out=k_sb[:, NB : NB + 8, :], in_=k_v[:, 0:8, :])
-        nc.sync.dma_start(out=x_sb[:, 4:8, :], in_=x_v[:, 4:8, :])
-        for g in range(1, 8):
-            nc.sync.dma_start(out=k_sb[:, NB + 8 * g : NB + 8 * g + 8, :], in_=k_v[:, 8 * g : 8 * g + 8, :])
-            nc.sync.dma_start(out=x_sb[:, 8 * g : 8 * g + 8, :], in_=x_v[:, 8 * g : 8 * g + 8, :])
-        for q in range(0, QB - 1):
-            nc.sync.dma_start(out=k_sb[q:P:QB, R + NB : HR, :], in_=k_h[:, q + 1, 0:NB, :])
-        with nc.allow_non_contiguous_dma(reason="bias, two neighbouring values to a partition"):
-            nc.scalar.dma_start(
-                out=b_cols[:].rearrange("w (u e) -> w u e", e=2),
-                in_=bq.rearrange("(u w e) -> w u e", u=2, e=2),
-            )
-
-        nc.vector.tensor_reduce(out=f_lo[:], in_=ident[:, 0:P:QB], axis=AX.X, op=ALU.add)
-        nc.vector.tensor_reduce(out=f_hi[:], in_=ident[:, QB - 1 : P : QB], axis=AX.X, op=ALU.add)
-        nc.vector.tensor_scalar_mul(out=f_lo[:], in0=f_lo[:], scalar1=NEG)
-        nc.vector.tensor_scalar_mul(out=f_hi[:], in0=f_hi[:], scalar1=NEG)
-
-        def quantise_four(words_of, codes, scales):
-            grouped = stage.tile([P, GROUP * P, 4], BF16, align_bytes=64, tag="grouped")
-            g32 = grouped[:].bitcast(F32)
-            for h in range(2):
-                xt = ps_xt.tile([P, 2, 2, P], F32, tag="xt")
-                for i in range(2):
-                    for u in range(2):
-                        nc.tensor.transpose(xt[:, i, u, :], words_of(2 * h + i)[:, u * P : (u + 1) * P], ident[:])
-                nc.scalar.copy(
-                    out=g32[:, 2 * h * P : (2 * h + 2) * P, :].rearrange("p (i t) u -> p i t u", i=2),
-                    in_=xt[:].rearrange("p i u t -> p i t u"),
-                )
-            nc.vector.quantize_mx(
-                out=codes.bitcast(FP8X4),
-                scales=scales,
-                in_=grouped[:].rearrange("p t j -> p (t j)"),
-            )
+        tiles = {
+            "tp": banks[0:2],
+            "qv": banks[2:5],
+            "qs": banks[5:7],
+            "grp": [keep.tile([P, 4 * P, 4], BF16, align_bytes=64, name="grp%d" % i) for i in range(2)],
+            "codes": [keep.tile([P, 4 * P], U32, align_bytes=64, name="codes%d" % i) for i in range(4)],
+            "ktsb": [keep.tile([P, 2, 2, P], F32, name="ktsb%d" % i) for i in range(2)],
+            "qsb": [keep.tile([P, D], F32, name="qsb%d" % i) for i in range(3)],
+            "prod": [keep.tile([P, W, D], F32, name="prod%d" % i) for i in range(3)],
+            "soft": [keep.tile([P, 2, 16, W], F32, name="soft%d" % i) for i in range(2)],
+        }
+        planes = [keep.tile([P, 4 * P], U8, align_bytes=64, name="planes%d" % i) for i in range(4)]
+        stats = [keep.tile([P, 2, 16], F32, name="stats%d" % i) for i in range(2)]
+        slots = {}
+        for name in tiles:
+            slots[name] = [0.0] * len(tiles[name])
 
         w32 = w_sb[:].bitcast(F32)
         x32 = x_sb[:].bitcast(F32)
         k32 = k_sb[:].bitcast(F32)
-        quantise_four(lambda i: w32[:, i, :], w_codes[:], w_scales[:])
 
-        c_ps = ps_c.tile([P, HR], F32)
+        tasks = []
 
-        def bias_dot(i0):
-            kt = ps_kt.tile([P, 2, 2, P], F32, tag="kt")
-            for i in range(2):
-                for u in range(2):
-                    nc.tensor.transpose(kt[:, i, u, :], k32[:, i0 + i, u * P : (u + 1) * P], ident[:])
-            kt_sb = stage.tile([P, 2, 2, P], F32, tag="kt_sb")
-            nc.scalar.copy(out=kt_sb[:], in_=kt[:])
-            kt_bf = kt_sb[:].bitcast(BF16).rearrange("p i u (t e) -> p i u t e", e=2)
-            for i in range(2):
-                for n in range(4):
-                    nc.tensor.matmul(
-                        out=c_ps[:, i0 + i : i0 + i + 1],
-                        lhsT=kt_bf[:, i, n // 2, :, n % 2],
-                        rhs=b_cols[:, n : n + 1],
-                        start=(n == 0),
-                        stop=(n == 3),
-                    )
+        def add(eng, dur, deps, emit, due, take=None, give=None):
+            tasks.append([eng, dur, deps, emit, due, take, give])
+            return len(tasks) - 1
 
-        def softmax(r0, r1):
-            n = r1 - r0
-            t1 = small.tile([P, SOFT, W], F32, tag="t1")
-            for j in range(W):
-                nc.vector.tensor_tensor(
-                    out=t1[:, 0:n, j], in0=sc[:, r0:r1, j], in1=c_sb[:, r0 + j : r1 + j], op=ALU.add
+        t_ident = add("G", 1.0, [], lambda: make_identity(nc, ident[:]), -100.0)
+
+        def emit_flags():
+            nc.vector.tensor_reduce(out=f_lo[:], in_=ident[:, 0:P:QB], axis=AX.X, op=ALU.add)
+            nc.vector.tensor_reduce(out=f_hi[:], in_=ident[:, QB - 1 : P : QB], axis=AX.X, op=ALU.add)
+            nc.vector.tensor_scalar_mul(out=f_lo[:], in0=f_lo[:], scalar1=NEG)
+            nc.vector.tensor_scalar_mul(out=f_hi[:], in0=f_hi[:], scalar1=NEG)
+
+        def emit_zero_halo():
+            nc.vector.memset(k_sb[:, 0:NB, :], 0.0)
+            nc.vector.memset(k_sb[:, R + NB : HR, :], 0.0)
+
+        t_zero = add("V", 0.5, [], emit_zero_halo, -100.0)
+        t_flags = add("V", 0.4, [t_ident], emit_flags, -50.0)
+
+        def due_tile(r):
+            return T_V * r if r < NV else T_G * (R - 1 - r)
+
+        def load(out_ap, in_ap):
+            return lambda: nc.sync.dma_start(out=out_ap, in_=in_ap)
+
+        t_w = add("D", 1.0, [], load(w_sb[:], Wq.rearrange("(c p) d -> p c d", p=P)), -30.0)
+
+        def emit_bias_load():
+            with nc.allow_non_contiguous_dma(reason="bias, two neighbouring values to a partition"):
+                nc.scalar.dma_start(
+                    out=b_cols[:].rearrange("w (u e) -> w u e", e=2),
+                    in_=bq.rearrange("(u w e) -> w u e", u=2, e=2),
                 )
-            for r, j0, j1, flag in ((0, 0, 2, f_lo), (1, 0, 1, f_lo), (R - 2, 4, 5, f_hi), (R - 1, 3, 5, f_hi)):
-                if r0 <= r < r1:
-                    nc.vector.tensor_scalar_add(
-                        out=t1[:, r - r0, j0:j1], in0=t1[:, r - r0, j0:j1], scalar1=flag[:, 0:1]
-                    )
-            mx = small.tile([P, SOFT], F32, tag="mx")
-            nc.vector.tensor_reduce(out=mx[:, 0:n], in_=t1[:, 0:n, :], axis=AX.X, op=ALU.max)
-            nc.vector.tensor_tensor(
-                out=t1[:, 0:n, :], in0=t1[:, 0:n, :], in1=mx[:, 0:n].unsqueeze(2).to_broadcast([P, n, W]), op=ALU.subtract
-            )
-            ex = small.tile([P, SOFT, W], F32, tag="ex")
-            nc.scalar.activation(out=ex[:, 0:n, :], in_=t1[:, 0:n, :], func=ACT.Exp)
-            sm = small.tile([P, SOFT], F32, tag="sm")
-            nc.vector.tensor_reduce(out=sm[:, 0:n], in_=ex[:, 0:n, :], axis=AX.X, op=ALU.add)
-            nc.vector.reciprocal(out=sm[:, 0:n], in_=sm[:, 0:n])
-            nc.vector.tensor_tensor(
-                out=out_sb[:, r0:r1, :], in0=ex[:, 0:n, :], in1=sm[:, 0:n].unsqueeze(2).to_broadcast([P, n, W]), op=ALU.mult
-            )
-            nc.sync.dma_start(out=out_v[:, r0:r1, :], in_=out_sb[:, r0:r1, :])
 
-        next_c = 0
-        c_copied = 0
-        soft_done = 0
-        for g in range(R // GROUP):
-            x_codes = stage.tile([P, GROUP * P], U32, align_bytes=64, tag="x_codes")
-            x_scales = stage.tile([P, GROUP * P], U8, align_bytes=64, tag="x_scales")
-            quantise_four(lambda i: x32[:, GROUP * g + i, :], x_codes[:], x_scales[:])
-            while next_c < min(HR, GROUP * g + 8):
-                bias_dot(next_c)
-                next_c += 2
-            for i in range(GROUP):
-                r = GROUP * g + i
-                q0 = ps_q.tile([P, D], F32, tag="q0")
+        t_b0 = add("S", 0.1, [], emit_bias_load, -100.0)
+        t_b = add("N", 4.0, [t_b0], None, 0.0)
+
+        t_x = {}
+        t_k = {}
+        for g in range(R // 4):
+            due = min(due_tile(4 * g), due_tile(4 * g + 3))
+            t_x[g] = add("D", 1.0, [], load(x_sb[:, 4 * g : 4 * g + 4, :], x_v[:, 4 * g : 4 * g + 4, :]), due - 20.0)
+            near = min(due_tile(max(0, 4 * g - 2)), due_tile(min(R - 1, 4 * g + 5)))
+            t_k[g] = add(
+                "D", 1.0, [], load(k_sb[:, NB + 4 * g : NB + 4 * g + 4, :], k_v[:, 4 * g : 4 * g + 4, :]), near - 19.0
+            )
+
+        def emit_halo_lo():
+            for q in range(1, QB):
+                nc.sync.dma_start(out=k_sb[q:P:QB, 0:NB, :], in_=k_h[:, q - 1, R - NB : R, :])
+
+        def emit_halo_hi():
+            for q in range(0, QB - 1):
+                nc.sync.dma_start(out=k_sb[q:P:QB, R + NB : HR, :], in_=k_h[:, q + 1, 0:NB, :])
+
+        t_hlo = add("D", 0.6, [t_zero], emit_halo_lo, due_tile(0) - 19.5)
+        t_hhi = add("D", 0.6, [t_zero], emit_halo_hi, due_tile(R - 1) - 19.5)
+        lat = {}
+        for name, t in (("w", t_w), ("hlo", t_hlo), ("hhi", t_hhi)):
+            lat[name] = add("N", 2.0, [t], None, 0.0)
+        for g in range(R // 4):
+            t_x[g] = add("N", 2.0, [t_x[g]], None, 0.0)
+            t_k[g] = add("N", 2.0, [t_k[g]], None, 0.0)
+
+        def key_row_loads(i0, i1):
+            deps = []
+            for i in range(i0, i1):
+                t = lat["hlo"] if i < NB else (lat["hhi"] if i >= R + NB else t_k[(i - NB) // 4])
+                if t not in deps:
+                    deps.append(t)
+            return deps
+
+        def quantise_four(words_of, deps, due, codes_of, copy_engine):
+            cx = {}
+            last = []
+            for h in range(2):
+                ch = {}
+
+                def emit_t(h=h, ch=ch):
+                    xt = tiles["tp"][ch["tp"]][:].rearrange("p (i u t) -> p i u t", i=2, u=2)
+                    for i in range(2):
+                        for u in range(2):
+                            nc.tensor.transpose(xt[:, i, u, :], words_of(2 * h + i)[:, u * P : (u + 1) * P], ident[:])
+
+                def emit_c(h=h, ch=ch):
+                    xt = tiles["tp"][ch["tp"]][:].rearrange("p (i u t) -> p i u t", i=2, u=2)
+                    g32 = tiles["grp"][cx["grp"]][:].bitcast(F32)
+                    dst = g32[:, 2 * h * P : (2 * h + 2) * P, :].rearrange("p (i t) u -> p i t u", i=2)
+                    src = xt.rearrange("p i u t -> p i t u")
+                    if copy_engine == "V":
+                        nc.vector.tensor_copy(out=dst, in_=src)
+                    else:
+                        nc.scalar.copy(out=dst, in_=src)
+
+                if h == 0:
+                    t_g = add("N", 0.0, [], None, due, take=("grp", cx))
+                t_t = add("T", 0.45, deps + [t_ident, t_g], emit_t, due, take=("tp", ch))
+                last.append(add(copy_engine, 0.46, [t_t], emit_c, due, give=("tp", ch)))
+
+            def emit_q():
+                codes, scales = codes_of(cx)
+                nc.vector.quantize_mx(
+                    out=codes[:].bitcast(FP8X4),
+                    scales=scales[:],
+                    in_=tiles["grp"][cx["grp"]][:].rearrange("p t j -> p (t j)"),
+                )
+
+            return cx, last, emit_q
+
+        cxw, lastw, emit_qw = quantise_four(lambda i: w32[:, i, :], [lat["w"]], -5000.0, lambda cx: (w_codes, w_scales), "V")
+        t_wq = add("V", 0.47, lastw, emit_qw, -5000.0, give=("grp", cxw))
+
+        t_q = {}
+        cx_q = {}
+        for g in range(R // 4):
+            due = min(due_tile(4 * g), due_tile(4 * g + 3)) - 1000.0
+            cxg, lastg, emit_qg = quantise_four(
+                lambda i, g=g: x32[:, 4 * g + i, :],
+                [t_x[g]],
+                due,
+                lambda cx: (tiles["codes"][cx["codes"]], planes[cx["codes"]]),
+                "S",
+            )
+            t_c = add("N", 0.0, lastg, None, due, take=("codes", cxg))
+            t_q[g] = add("V", 0.47, [t_c], emit_qg, due, give=("grp", cxg))
+            cx_q[g] = cxg
+
+        def emit_mx(r, pool, ct):
+            def emit():
+                cxg = cx_q[r // 4]
+                i = r % 4
                 nc.tensor.matmul_mx(
-                    out=q0[:],
-                    lhsT=x_codes[:, i * P : (i + 1) * P].bitcast(FP8X4),
-                    lhsT_scale=x_scales[:, i * P : (i + 1) * P],
+                    out=tiles[pool][ct[pool]][:],
+                    lhsT=tiles["codes"][cxg["codes"]][:, i * P : (i + 1) * P].bitcast(FP8X4),
+                    lhsT_scale=planes[cxg["codes"]][:, i * P : (i + 1) * P],
                     rhs=w_codes[:].bitcast(FP8X4),
                     rhs_scale=w_scales[:],
                     start=True,
                     stop=True,
                 )
-                if r in G_TILES:
-                    q_sb = gpool.tile([P, D], F32, tag="q_sb")
-                    nc.scalar.mul(out=q_sb[:], in_=q0[:], mul=SCALE)
-                    prod = gpool.tile([P, W, D], F32, tag="prod")
-                    nc.gpsimd.tensor_tensor(
-                        out=prod[:],
-                        in0=q_sb[:].unsqueeze(1).to_broadcast([P, W, D]),
-                        in1=k_sb[:, r : r + W, :],
-                        op=ALU.mult,
-                    )
+
+            return emit
+
+        t_mx = {}
+        t_done = {}
+        for r in range(R):
+            ct = {}
+            due = due_tile(r)
+            rows = key_row_loads(r, r + W)
+            if r < NV:
+                t_mx[r] = add("T", 0.23, [t_q[r // 4], t_wq], emit_mx(r, "qv", ct), due - 1000.0, take=("qv", ct))
+
+                def emit_v(r=r, ct=ct):
                     for j in range(W):
-                        s_junk = stage.tile([P, D], BF16, tag="s_junk")
-                        nc.scalar.activation(
-                            out=s_junk[:], in_=prod[:, j, :], func=ACT.Copy, accum_out=sc[:, r, j : j + 1]
-                        )
-                else:
-                    for j in range(W):
-                        v_junk = stage.tile([P, D], F32, tag="v_junk")
                         nc.vector.scalar_tensor_tensor(
                             out=v_junk[:],
-                            in0=q0[:],
+                            in0=tiles["qv"][ct["qv"]][:],
                             scalar=SCALE,
                             in1=k_sb[:, r + j, :],
                             op0=ALU.mult,
                             op1=ALU.mult,
                             accum_out=sc[:, r, j : j + 1],
                         )
-            done = GROUP * (g + 1)
-            if done in SOFT_ENDS:
-                nc.scalar.mul(out=c_sb[:, c_copied : done + 4], in_=c_ps[:, c_copied : done + 4], mul=SCALE)
-                c_copied = done + 4
-                softmax(soft_done, done)
-                soft_done = done
+
+                t_done[r] = [add("V", T_V, [t_mx[r]] + rows, emit_v, due, give=("qv", ct))]
+            else:
+                t_mx[r] = add("T", 0.23, [t_q[r // 4], t_wq], emit_mx(r, "qs", ct), due - 500.0, take=("qs", ct))
+                t_s = add("N", 0.0, [t_mx[r]], None, due - 500.0, take=("qsb", ct))
+
+                def emit_e(ct=ct):
+                    nc.scalar.mul(out=tiles["qsb"][ct["qsb"]][:], in_=tiles["qs"][ct["qs"]][:], mul=SCALE)
+
+                t_e = add("S", 0.46, [t_s], emit_e, due - 500.0, give=("qs", ct))
+                t_p = add("N", 0.0, [t_e], None, due, take=("prod", ct))
+
+                def emit_g(r=r, ct=ct):
+                    nc.gpsimd.tensor_tensor(
+                        out=tiles["prod"][ct["prod"]][:],
+                        in0=tiles["qsb"][ct["qsb"]][:].unsqueeze(1).to_broadcast([P, W, D]),
+                        in1=k_sb[:, r : r + W, :],
+                        op=ALU.mult,
+                    )
+
+                t_g = add("G", T_G, [t_p] + rows, emit_g, due, give=("qsb", ct))
+                sums = []
+                for j in range(W):
+
+                    def emit_r(r=r, j=j, ct=ct):
+                        nc.scalar.activation(
+                            out=s_junk[:],
+                            in_=tiles["prod"][ct["prod"]][:, j, :],
+                            func=ACT.Copy,
+                            accum_out=sc[:, r, j : j + 1],
+                        )
+
+                    sums.append(add("S", 0.53, [t_g], emit_r, due + T_G + 0.5 * j))
+                add("N", 0.0, sums, None, 0.0, give=("prod", ct))
+                t_done[r] = sums
+        for g in range(R // 4):
+            add("N", 0.0, [t_mx[4 * g + i] for i in range(4)], None, 0.0, give=("codes", cx_q[g]))
+
+        t_cm = []
+        for i0 in range(0, HR, 2):
+            ck = {}
+            due = 3000.0 + i0
+
+            def emit_kt(i0=i0, ck=ck):
+                kt = tiles["tp"][ck["tp"]][:].rearrange("p (i u t) -> p i u t", i=2, u=2)
+                for i in range(2):
+                    for u in range(2):
+                        nc.tensor.transpose(kt[:, i, u, :], k32[:, i0 + i, u * P : (u + 1) * P], ident[:])
+
+            def emit_kc(ck=ck):
+                nc.scalar.copy(
+                    out=tiles["ktsb"][ck["ktsb"]][:].rearrange("p i u t -> p (i u t)"), in_=tiles["tp"][ck["tp"]][:]
+                )
+
+            def emit_cm(i0=i0, ck=ck):
+                kt_bf = tiles["ktsb"][ck["ktsb"]][:].bitcast(BF16).rearrange("p i u (t e) -> p i u t e", e=2)
+                for i in range(2):
+                    for n in range(4):
+                        nc.tensor.matmul(
+                            out=c_ps[:, i0 + i : i0 + i + 1],
+                            lhsT=kt_bf[:, i, n // 2, :, n % 2],
+                            rhs=b_cols[:, n : n + 1],
+                            start=(n == 0),
+                            stop=(n == 3),
+                        )
+
+            t_s = add("N", 0.0, key_row_loads(i0, i0 + 2) + [t_ident], None, due, take=("ktsb", ck))
+            t_t = add("T", 0.45, [t_s], emit_kt, due, take=("tp", ck))
+            t_c = add("S", 0.46, [t_t], emit_kc, due, give=("tp", ck))
+            t_cm.append(add("T", 0.5, [t_c, t_b], emit_cm, due, give=("ktsb", ck)))
+        t_csb = add("S", 0.15, t_cm, lambda: nc.scalar.mul(out=c_sb[:], in_=c_ps[:, 0:HR], mul=SCALE), -1000.0)
+
+        def softmax(r0, r1, due):
+            n = r1 - r0
+            cs = {}
+            deps = [t_csb, t_flags]
+            for r in range(r0, r1):
+                deps.extend(t_done[r])
+
+            def emit_a():
+                t1 = tiles["soft"][cs["soft"]][:, 0, 0:n, :]
+                mx = stats[cs["soft"]][:, 0, 0:n]
+                for j in range(W):
+                    nc.vector.tensor_tensor(out=t1[:, :, j], in0=sc[:, r0:r1, j], in1=c_sb[:, r0 + j : r1 + j], op=ALU.add)
+                for r, j0, j1, flag in ((0, 0, 2, f_lo), (1, 0, 1, f_lo), (R - 2, 4, 5, f_hi), (R - 1, 3, 5, f_hi)):
+                    if r0 <= r < r1:
+                        nc.vector.tensor_scalar_add(
+                            out=t1[:, r - r0, j0:j1], in0=t1[:, r - r0, j0:j1], scalar1=flag[:, 0:1]
+                        )
+                nc.vector.tensor_reduce(out=mx, in_=t1, axis=AX.X, op=ALU.max)
+                nc.vector.tensor_tensor(out=t1, in0=t1, in1=mx.unsqueeze(2).to_broadcast([P, n, W]), op=ALU.subtract)
+
+            def emit_e():
+                both = tiles["soft"][cs["soft"]]
+                nc.scalar.activation(out=both[:, 1, 0:n, :], in_=both[:, 0, 0:n, :], func=ACT.Exp)
+
+            def emit_n():
+                ex = tiles["soft"][cs["soft"]][:, 1, 0:n, :]
+                sm = stats[cs["soft"]][:, 1, 0:n]
+                nc.vector.tensor_reduce(out=sm, in_=ex, axis=AX.X, op=ALU.add)
+                nc.vector.reciprocal(out=sm, in_=sm)
+                nc.vector.tensor_tensor(
+                    out=out_sb[:, r0:r1, :], in0=ex, in1=sm.unsqueeze(2).to_broadcast([P, n, W]), op=ALU.mult
+                )
+
+            t_a = add("V", 0.9, deps, emit_a, -500.0, take=("soft", cs))
+            t_e = add("S", 0.2, [t_a], emit_e, -1000.0)
+            t_n = add("V", 0.4, [t_e], emit_n, -500.0, give=("soft", cs))
+            add("D", 0.2, [t_n], lambda: nc.sync.dma_start(out=out_v[:, r0:r1, :], in_=out_sb[:, r0:r1, :]), due)
+
+        for r0, r1 in V_CHUNKS:
+            softmax(r0, r1, max(50.0, due_tile(r1 - 1) + T_V))
+        for r0, r1 in G_CHUNKS:
+            softmax(r0, r1, max(50.0, due_tile(r0) + 2 * T_G))
+
+        run_schedule(tasks, slots)

@@ -104,8 +104,8 @@ def tile_crosssliceattention_pa_t_kernel(tc, x, Wq, bq, k_proj, out):
         out_sb = keep.tile([P, R, W], F32, name="out_sb")
         f_lo = keep.tile([P, 1], F32, name="f_lo")
         f_hi = keep.tile([P, 1], F32, name="f_hi")
-        v_junk = keep.tile([P, D], F32, name="v_junk")
-        s_junk = keep.tile([P, D], BF16, name="s_junk")
+        v_junk = [keep.tile([P, D], F32, name="v_junk%d" % i) for i in range(5)]
+        s_junk = [keep.tile([P, D], BF16, name="s_junk%d" % i) for i in range(5)]
         banks = [psum.tile([P, 512], F32, name="bank%d" % i) for i in range(8)]
         c_ps = banks[7]
 
@@ -287,7 +287,7 @@ def tile_crosssliceattention_pa_t_kernel(tc, x, Wq, bq, k_proj, out):
                 def emit_v(r=r, ct=ct):
                     for j in range(W):
                         nc.vector.scalar_tensor_tensor(
-                            out=v_junk[:],
+                            out=v_junk[j][:],
                             in0=tiles["qv"][ct["qv"]][:],
                             scalar=SCALE,
                             in1=k_sb[:, r + j, :],
@@ -321,7 +321,7 @@ def tile_crosssliceattention_pa_t_kernel(tc, x, Wq, bq, k_proj, out):
 
                     def emit_r(r=r, j=j, ct=ct):
                         nc.scalar.activation(
-                            out=s_junk[:],
+                            out=s_junk[j][:],
                             in_=tiles["prod"][ct["prod"]][:, j, :],
                             func=ACT.Copy,
                             accum_out=sc[:, r, j : j + 1],

@@ -6,6 +6,7 @@ from concourse.masks import make_identity
 
 F32 = mybir.dt.float32
 BF16 = mybir.dt.bfloat16
+I32 = mybir.dt.int32
 U32 = mybir.dt.uint32
 U8 = mybir.dt.uint8
 FP8X4 = mybir.dt.float8_e4m3fn_x4
@@ -17,18 +18,32 @@ P = 128
 B, S, D = 32, 256, 512
 W = 5
 NB = 2
-R = 64
-QB = S // R
-HR = R + 2 * NB
 SCALE = 1.0 / math.sqrt(D)
 NEG = -1.0e30
-NG = 24
+
+T_RANGES = ((0, 6), (26, 32))
+T_BATCHES = tuple(range(0, 6)) + tuple(range(26, 32))
+NPAIR = len(T_BATCHES) // 2
+NTT = 2 * len(T_BATCHES)
+BW = P + 2 * NB
+V_B0, V_NB = 6, 20
+R = V_NB * S // P
+HR = R + 2 * NB
+TOK0 = V_B0 * S
+NTOK = V_NB * S
+NG = 10
 NV = R - NG
-V_CHUNKS = ((0, 16), (16, 32), (32, NV - 2), (NV - 2, NV))
-G_CHUNKS = ((52, 64), (NV + 3, 52), (NV, NV + 3))
+V_CHUNKS = ((0, 14), (14, NV - 2), (NV - 2, NV))
+G_CHUNKS = ((NV + 2, R), (NV, NV + 2))
 
 T_V = 2.35
-T_G = 4.45
+T_G = 5.25
+G_SPLIT = ((0, 1), (1, 2), (2, 3), (3, 4), (4, 5))
+G_START = 22.0
+PACE_G = 5.3
+PACE_P = 10.5
+NX = R // 4 + NPAIR
+LAT = 0.3
 LOG = []
 
 FLOPS = 2 * B * S * D * D + 2 * B * S * W * D
@@ -49,7 +64,7 @@ def run_schedule(tasks, slots):
                 if fin[d] < 0.0:
                     ok = False
                     break
-                est = max(est, fin[d])
+                est = max(est, fin[d] + (LAT if tasks[d][0] not in ("N", eng) else 0.0))
             if not ok:
                 continue
             if take is not None:
@@ -65,15 +80,14 @@ def run_schedule(tasks, slots):
         eng, dur, deps, emit, due, take, give = tasks[i]
         if take is not None:
             pool = slots[take[0]]
-            free = min(f for f in pool if f >= 0.0)
-            k = pool.index(free)
+            k = pool.index(min(f for f in pool if f >= 0.0))
             pool[k] = -1.0
             take[1][take[0]] = k
         fin[i] = est + dur
         if eng in busy:
             busy[eng] = fin[i]
-        if give is not None:
-            slots[give[0]][give[1][give[0]]] = fin[i]
+        for g in give:
+            slots[g[0]][g[1][g[0]]] = fin[i] + LAT
         if emit is not None:
             emit()
         LOG.append((eng, est, fin[i], i))
@@ -82,82 +96,142 @@ def run_schedule(tasks, slots):
 
 def tile_crosssliceattention_pa_t_kernel(tc, x, Wq, bq, k_proj, out):
     nc = tc.nc
-    x_v = x.rearrange("b (q r) d -> (b q) r d", r=R)
-    k_v = k_proj.rearrange("b (q r) d -> (b q) r d", r=R)
-    k_h = k_proj.rearrange("b (q r) d -> b q r d", r=R)
-    out_v = out.rearrange("b (q r) j -> (b q) r j", r=R)
+    x_f = x.flatten_outer_dims()
+    k_f = k_proj.flatten_outer_dims()
+    out_f = out.flatten_outer_dims()
+    x_v = x_f[TOK0 : TOK0 + NTOK, :].rearrange("(p r) d -> p r d", r=R)
+    k_lo = k_f[TOK0 - NB : TOK0 - NB + NTOK, :].rearrange("(p r) d -> p r d", r=R)
+    k_hi = k_f[TOK0 - NB + R : TOK0 - NB + R + NTOK, :].rearrange("(p r) d -> p r d", r=R)
+    out_v = out_f[TOK0 : TOK0 + NTOK, :].rearrange("(p r) j -> p r j", r=R)
 
     with ExitStack() as ctx:
         keep = ctx.enter_context(tc.tile_pool(name="keep", bufs=1))
         psum = ctx.enter_context(tc.psum_pool(name="psum", bufs=1))
         ctx.enter_context(tc.manual_schedule())
 
+        def many(n, shape, dtype, name, align=None):
+            if align is None:
+                return [keep.tile(shape, dtype, name="%s%d" % (name, i)) for i in range(n)]
+            return [keep.tile(shape, dtype, align_bytes=align, name="%s%d" % (name, i)) for i in range(n)]
+
         ident = keep.tile([P, P], F32, name="ident")
-        x_sb = keep.tile([P, R, D], BF16, name="x_sb")
+        ident_bf = keep.tile([P, P], BF16, name="ident_bf")
+        codes_all = keep.tile([P, NX, 4 * P], U32, align_bytes=64, name="codes_all")
+        planes_all = keep.tile([P, NX, 4 * P], U8, align_bytes=64, name="planes_all")
         k_sb = keep.tile([P, HR, D], BF16, name="k_sb")
         w_sb = keep.tile([P, 4, D], BF16, name="w_sb")
         b_cols = keep.tile([P, 4], BF16, name="b_cols")
+        b_rows = keep.tile([P, P], BF16, name="b_rows")
+        b_nat = keep.tile([P, 4], F32, name="b_nat")
         w_codes = keep.tile([P, D], U32, align_bytes=64, name="w_codes")
         w_scales = keep.tile([P, D], U8, align_bytes=64, name="w_scales")
         sc = keep.tile([P, R, 8], F32, name="sc")
         c_sb = keep.tile([P, HR], F32, name="c_sb")
+        cm = keep.tile([P, R, W], F32, name="cm")
+        mask = keep.tile([P, R, W], F32, name="mask")
+        idx = keep.tile([P, R], I32, name="idx")
+        loc = keep.tile([P, R], F32, name="loc")
         out_sb = keep.tile([P, R, W], F32, name="out_sb")
-        f_lo = keep.tile([P, 1], F32, name="f_lo")
-        f_hi = keep.tile([P, 1], F32, name="f_hi")
-        v_junk = [keep.tile([P, D], F32, name="v_junk%d" % i) for i in range(5)]
-        s_junk = [keep.tile([P, D], BF16, name="s_junk%d" % i) for i in range(5)]
+        band01 = keep.tile([P, BW], F32, name="band01")
+        sel = keep.tile([P, W], F32, name="sel")
+        mask_t = keep.tile([P, 2, W], F32, name="mask_t")
+        er2 = keep.tile([P, NTT, 2 * W], F32, name="er2")
+        e_t = keep.tile([P, NTT, W], F32, name="e_t")
+        x_t = keep.tile([P, NTT, W], F32, name="x_t")
+        st_t = keep.tile([P, 2, NTT], F32, name="st_t")
+        p_t = keep.tile([P, 2, P], F32, name="p_t")
+        t1_sb = keep.tile([P, 2 * P], F32, name="t1_sb")
+        f_sb = keep.tile([P, NTT // 2, 2, W], F32, name="f_sb")
+        v_junk = many(5, [P, D], F32, "v_junk")
+        s_junk = many(5, [P, D], BF16, "s_junk")
         banks = [psum.tile([P, 512], F32, name="bank%d" % i) for i in range(8)]
-        c_ps = banks[7]
+        c_ps = banks[6][:, 2 * BW : 2 * BW + HR]
 
         tiles = {
-            "tp": banks[0:2],
-            "qv": banks[2:5],
-            "qs": banks[5:7],
-            "grp": [keep.tile([P, 4 * P, 4], BF16, align_bytes=64, name="grp%d" % i) for i in range(2)],
-            "codes": [keep.tile([P, 4 * P], U32, align_bytes=64, name="codes%d" % i) for i in range(4)],
-            "ktsb": [keep.tile([P, 2, 2, P], F32, name="ktsb%d" % i) for i in range(2)],
-            "qsb": [keep.tile([P, D], F32, name="qsb%d" % i) for i in range(3)],
-            "prod": [keep.tile([P, W, D], F32, name="prod%d" % i) for i in range(3)],
-            "soft": [keep.tile([P, 2, 16, W], F32, name="soft%d" % i) for i in range(2)],
+            "ps": [banks[0], banks[1], banks[4], banks[5]],
+            "qv": [banks[2], banks[3], banks[7]],
+            "sps": banks[6:7],
+            "grp": many(3, [P, 4 * P, 4], BF16, "grp", 64),
+            "ktsb": many(2, [P, 2, 2, P], F32, "ktsb"),
+            "qsb": many(3, [P, D], F32, "qsb"),
+            "prod": many(2, [P, W, D], F32, "prod"),
+            "soft": many(2, [P, 2, 16, W], F32, "soft"),
+            "xs": many(6, [P, 4, D], BF16, "xs"),
+            "kb": many(2, [P, 4, D], BF16, "kb"),
+            "qT": many(2, [P, 4, 4 * P], F32, "qT"),
+            "kT": many(3, [P, 4, S + 2 * NB], F32, "kT"),
+            "mk": many(2, [P, 2, BW + 3], F32, "mk"),
         }
-        planes = [keep.tile([P, 4 * P], U8, align_bytes=64, name="planes%d" % i) for i in range(4)]
-        stats = [keep.tile([P, 2, 16], F32, name="stats%d" % i) for i in range(2)]
+        stats = many(2, [P, 2, 16], F32, "stats")
         slots = {}
         for name in tiles:
             slots[name] = [0.0] * len(tiles[name])
 
         w32 = w_sb[:].bitcast(F32)
-        x32 = x_sb[:].bitcast(F32)
         k32 = k_sb[:].bitcast(F32)
 
         tasks = []
 
-        def add(eng, dur, deps, emit, due, take=None, give=None):
+        def add(eng, dur, deps, emit, due, take=None, give=()):
             tasks.append([eng, dur, deps, emit, due, take, give])
             return len(tasks) - 1
-
-        t_ident = add("G", 1.0, [], lambda: make_identity(nc, ident[:]), -100.0)
-
-        def emit_flags():
-            nc.vector.tensor_reduce(out=f_lo[:], in_=ident[:, 0:P:QB], axis=AX.X, op=ALU.add)
-            nc.vector.tensor_reduce(out=f_hi[:], in_=ident[:, QB - 1 : P : QB], axis=AX.X, op=ALU.add)
-            nc.vector.tensor_scalar_mul(out=f_lo[:], in0=f_lo[:], scalar1=NEG)
-            nc.vector.tensor_scalar_mul(out=f_hi[:], in0=f_hi[:], scalar1=NEG)
-
-        def emit_zero_halo():
-            nc.vector.memset(k_sb[:, 0:NB, :], 0.0)
-            nc.vector.memset(k_sb[:, R + NB : HR, :], 0.0)
-
-        t_zero = add("V", 0.5, [], emit_zero_halo, -100.0)
-        t_flags = add("V", 0.4, [t_ident], emit_flags, -50.0)
-
-        def due_tile(r):
-            return T_V * r if r < NV else T_G * (R - 1 - r)
 
         def load(out_ap, in_ap):
             return lambda: nc.sync.dma_start(out=out_ap, in_=in_ap)
 
-        t_w = add("D", 1.0, [], load(w_sb[:], Wq.rearrange("(c p) d -> p c d", p=P)), -30.0)
+        t_ident = add("G", 1.0, [], lambda: make_identity(nc, ident[:]), -9000.0)
+        t_iota = add(
+            "G", 0.3, [], lambda: nc.gpsimd.iota(idx[:], pattern=[[1, R]], base=0, channel_multiplier=R), -8900.0
+        )
+
+        def emit_band():
+            nc.gpsimd.memset(band01[:], 0.0)
+            for j in range(W):
+                nc.gpsimd.tensor_tensor(out=band01[:, j : j + P], in0=band01[:, j : j + P], in1=ident[:], op=ALU.add)
+
+        t_band = add("G", 2.0, [t_ident], emit_band, -8800.0)
+
+        def emit_zero_g():
+            for t in tiles["kT"]:
+                nc.gpsimd.memset(t[:], 0.0)
+            for t in tiles["mk"]:
+                nc.gpsimd.memset(t[:], 0.0)
+            nc.gpsimd.memset(p_t[:], 0.0)
+
+        t_zero = add("G", 4.0, [], emit_zero_g, -8700.0)
+
+        def emit_consts_v():
+            nc.vector.memset(b_rows[:], 0.0)
+            nc.vector.memset(mask[:], 0.0)
+            nc.vector.memset(mask_t[:], 0.0)
+
+        t_cv0 = add("V", 0.4, [], emit_consts_v, -9000.0)
+
+        def emit_masks():
+            nc.vector.tensor_copy(out=ident_bf[:], in_=ident[:])
+            for m in range(W):
+                nc.vector.tensor_reduce(out=sel[:, m : m + 1], in_=ident[:, m:P:W], axis=AX.X, op=ALU.add)
+            nc.vector.tensor_reduce(out=mask_t[:, 0, 0:1], in_=ident[:, 0:2], axis=AX.X, op=ALU.add)
+            nc.vector.tensor_copy(out=mask_t[:, 0, 1:2], in_=ident[:, 0:1])
+            nc.vector.tensor_copy(out=mask_t[:, 1, 3:4], in_=ident[:, P - 1 : P])
+            nc.vector.tensor_reduce(out=mask_t[:, 1, 4:5], in_=ident[:, P - 2 : P], axis=AX.X, op=ALU.add)
+            nc.vector.tensor_scalar_mul(out=mask_t[:], in0=mask_t[:], scalar1=NEG)
+
+        t_masks = add("V", 1.2, [t_ident, t_cv0], emit_masks, -8900.0)
+
+        def emit_mask_v():
+            nc.vector.tensor_single_scalar(out=idx[:], in_=idx[:], scalar=S - 1, op=ALU.bitwise_and)
+            nc.vector.tensor_copy(out=loc[:], in_=idx[:])
+            for j, op, lim in ((0, ALU.is_lt, 2.0), (1, ALU.is_lt, 1.0), (3, ALU.is_gt, S - 2.0), (4, ALU.is_gt, S - 3.0)):
+                nc.vector.tensor_scalar(out=mask[:, :, j], in0=loc[:], scalar1=lim, scalar2=NEG, op0=op, op1=ALU.mult)
+
+        t_mask = add("V", 0.7, [t_iota, t_cv0], emit_mask_v, -8800.0)
+
+        def due_tile(r):
+            return 8.0 + T_V * 1.25 * r if r < NV else G_START + PACE_G * (R - 1 - r)
+
+        t_w = add("D", 1.0, [], load(w_sb[:], Wq.rearrange("(c p) d -> p c d", p=P)), -9000.0)
+        t_w = add("N", 2.0, [t_w], None, 0.0)
 
         def emit_bias_load():
             with nc.allow_non_contiguous_dma(reason="bias, two neighbouring values to a partition"):
@@ -165,59 +239,41 @@ def tile_crosssliceattention_pa_t_kernel(tc, x, Wq, bq, k_proj, out):
                     out=b_cols[:].rearrange("w (u e) -> w u e", e=2),
                     in_=bq.rearrange("(u w e) -> w u e", u=2, e=2),
                 )
+            nc.scalar.dma_start(out=b_rows[0:4, :], in_=bq.rearrange("(c p) -> c p", p=P))
 
-        t_b0 = add("S", 0.1, [], emit_bias_load, -100.0)
-        t_b = add("N", 4.0, [t_b0], None, 0.0)
+        t_b = add("S", 0.2, [t_cv0], emit_bias_load, -9000.0)
+        t_b = add("N", 4.0, [t_b], None, 0.0)
 
-        t_x = {}
         t_k = {}
-        for g in range(R // 4):
-            due = min(due_tile(4 * g), due_tile(4 * g + 3))
-            t_x[g] = add("D", 1.0, [], load(x_sb[:, 4 * g : 4 * g + 4, :], x_v[:, 4 * g : 4 * g + 4, :]), due - 20.0)
-            near = min(due_tile(max(0, 4 * g - 2)), due_tile(min(R - 1, 4 * g + 5)))
-            t_k[g] = add(
-                "D", 1.0, [], load(k_sb[:, NB + 4 * g : NB + 4 * g + 4, :], k_v[:, 4 * g : 4 * g + 4, :]), near - 19.0
-            )
-
-        def emit_halo_lo():
-            for q in range(1, QB):
-                nc.sync.dma_start(out=k_sb[q:P:QB, 0:NB, :], in_=k_h[:, q - 1, R - NB : R, :])
-
-        def emit_halo_hi():
-            for q in range(0, QB - 1):
-                nc.sync.dma_start(out=k_sb[q:P:QB, R + NB : HR, :], in_=k_h[:, q + 1, 0:NB, :])
-
-        t_hlo = add("D", 0.6, [t_zero], emit_halo_lo, due_tile(0) - 19.5)
-        t_hhi = add("D", 0.6, [t_zero], emit_halo_hi, due_tile(R - 1) - 19.5)
-        lat = {}
-        for name, t in (("w", t_w), ("hlo", t_hlo), ("hhi", t_hhi)):
-            lat[name] = add("N", 2.0, [t], None, 0.0)
-        for g in range(R // 4):
-            t_x[g] = add("N", 2.0, [t_x[g]], None, 0.0)
-            t_k[g] = add("N", 2.0, [t_k[g]], None, 0.0)
+        for g in range(HR // 4):
+            near = min(due_tile(max(0, 4 * g - 4)), due_tile(min(R - 1, 4 * g + 3)))
+            src = k_lo[:, 4 * g : 4 * g + 4, :] if g < R // 4 else k_hi[:, 0:4, :]
+            t = add("D", 1.0, [], load(k_sb[:, 4 * g : 4 * g + 4, :], src), near - 6.0)
+            t_k[g] = add("N", 2.0, [t], None, 0.0)
 
         def key_row_loads(i0, i1):
             deps = []
             for i in range(i0, i1):
-                t = lat["hlo"] if i < NB else (lat["hhi"] if i >= R + NB else t_k[(i - NB) // 4])
-                if t not in deps:
-                    deps.append(t)
+                if t_k[i // 4] not in deps:
+                    deps.append(t_k[i // 4])
             return deps
 
-        def quantise_four(words_of, deps, due, codes_of, copy_engine):
+        def quantise_four(words_of, deps, due, copy_engine):
             cx = {}
-            last = []
+            t_ts = []
+            t_cs = []
+            t_g = add("N", 0.0, deps, None, due, take=("grp", cx))
             for h in range(2):
                 ch = {}
 
                 def emit_t(h=h, ch=ch):
-                    xt = tiles["tp"][ch["tp"]][:].rearrange("p (i u t) -> p i u t", i=2, u=2)
+                    xt = tiles["ps"][ch["ps"]][:].rearrange("p (i u t) -> p i u t", i=2, u=2)
                     for i in range(2):
                         for u in range(2):
                             nc.tensor.transpose(xt[:, i, u, :], words_of(2 * h + i)[:, u * P : (u + 1) * P], ident[:])
 
                 def emit_c(h=h, ch=ch):
-                    xt = tiles["tp"][ch["tp"]][:].rearrange("p (i u t) -> p i u t", i=2, u=2)
+                    xt = tiles["ps"][ch["ps"]][:].rearrange("p (i u t) -> p i u t", i=2, u=2)
                     g32 = tiles["grp"][cx["grp"]][:].bitcast(F32)
                     dst = g32[:, 2 * h * P : (2 * h + 2) * P, :].rearrange("p (i t) u -> p i t u", i=2)
                     src = xt.rearrange("p i u t -> p i t u")
@@ -226,47 +282,62 @@ def tile_crosssliceattention_pa_t_kernel(tc, x, Wq, bq, k_proj, out):
                     else:
                         nc.scalar.copy(out=dst, in_=src)
 
-                if h == 0:
-                    t_g = add("N", 0.0, [], None, due, take=("grp", cx))
-                t_t = add("T", 0.45, deps + [t_ident, t_g], emit_t, due, take=("tp", ch))
-                last.append(add(copy_engine, 0.46, [t_t], emit_c, due, give=("tp", ch)))
+                t_ts.append(add("T", 0.45, [t_ident, t_g], emit_t, due, take=("ps", ch)))
+                t_cs.append(add(copy_engine, 0.46, [t_ts[h]], emit_c, due, give=(("ps", ch),)))
+            return cx, t_ts, t_cs
 
-            def emit_q():
-                codes, scales = codes_of(cx)
+        def emit_quant(cx, codes_of):
+            def emit():
+                codes, scales = codes_of()
                 nc.vector.quantize_mx(
-                    out=codes[:].bitcast(FP8X4),
-                    scales=scales[:],
+                    out=codes.bitcast(FP8X4),
+                    scales=scales,
                     in_=tiles["grp"][cx["grp"]][:].rearrange("p t j -> p (t j)"),
                 )
 
-            return cx, last, emit_q
+            return emit
 
-        cxw, lastw, emit_qw = quantise_four(lambda i: w32[:, i, :], [lat["w"]], -5000.0, lambda cx: (w_codes, w_scales), "V")
-        t_wq = add("V", 0.47, lastw, emit_qw, -5000.0, give=("grp", cxw))
+        cxw, tsw, csw = quantise_four(lambda i: w32[:, i, :], [t_w], -9000.0, "V")
+        t_wq = add("V", 0.47, csw, emit_quant(cxw, lambda: (w_codes[:], w_scales[:])), -9000.0, give=(("grp", cxw),))
 
-        t_q = {}
-        cx_q = {}
-        for g in range(R // 4):
-            due = min(due_tile(4 * g), due_tile(4 * g + 3)) - 1000.0
-            cxg, lastg, emit_qg = quantise_four(
-                lambda i, g=g: x32[:, 4 * g + i, :],
-                [t_x[g]],
+        def x_group(e, src, seq):
+            c0 = {}
+            t = add("D", 1.0, [], lambda: nc.sync.dma_start(out=tiles["xs"][c0["xs"]][:], in_=src), 0.5 * seq, take=("xs", c0))
+            t = add("N", 2.0, [t], None, 0.0)
+            due = -7000.0 + seq
+            cx, t_ts, t_cs = quantise_four(lambda i: tiles["xs"][c0["xs"]][:].bitcast(F32)[:, i, :], [t], due, "S")
+            add("N", 0.0, t_ts, None, 0.0, give=(("xs", c0),))
+            return add(
+                "V",
+                0.47,
+                t_cs,
+                emit_quant(cx, lambda: (codes_all[:, e, :], planes_all[:, e, :])),
                 due,
-                lambda cx: (tiles["codes"][cx["codes"]], planes[cx["codes"]]),
-                "S",
+                give=(("grp", cx),),
             )
-            t_c = add("N", 0.0, lastg, None, due, take=("codes", cxg))
-            t_q[g] = add("V", 0.47, [t_c], emit_qg, due, give=("grp", cxg))
-            cx_q[g] = cxg
+
+        order = []
+        for n in range(max(R // 4, NPAIR)):
+            if n < R // 4:
+                order.append(("v", n))
+            if n < NPAIR:
+                order.append(("t", n))
+        t_q = {}
+        t_qp = {}
+        for seq, (kind, n) in enumerate(order):
+            if kind == "v":
+                t_q[n] = x_group(n, x_v[:, 4 * n : 4 * n + 4, :], seq)
+            else:
+                b0 = T_BATCHES[2 * n]
+                t_qp[n] = x_group(R // 4 + n, x[b0 : b0 + 2].rearrange("b (h p) d -> p (b h) d", p=P), seq)
 
         def emit_mx(r, pool, ct):
             def emit():
-                cxg = cx_q[r // 4]
                 i = r % 4
                 nc.tensor.matmul_mx(
                     out=tiles[pool][ct[pool]][:],
-                    lhsT=tiles["codes"][cxg["codes"]][:, i * P : (i + 1) * P].bitcast(FP8X4),
-                    lhsT_scale=planes[cxg["codes"]][:, i * P : (i + 1) * P],
+                    lhsT=codes_all[:, r // 4, i * P : (i + 1) * P].bitcast(FP8X4),
+                    lhsT_scale=planes_all[:, r // 4, i * P : (i + 1) * P],
                     rhs=w_codes[:].bitcast(FP8X4),
                     rhs_scale=w_scales[:],
                     start=True,
@@ -277,15 +348,25 @@ def tile_crosssliceattention_pa_t_kernel(tc, x, Wq, bq, k_proj, out):
 
         t_mx = {}
         t_done = {}
-        for r in range(R):
+        prev_g = []
+        for r in list(range(NV)) + list(range(R - 1, NV - 1, -1)):
             ct = {}
             due = due_tile(r)
             rows = key_row_loads(r, r + W)
             if r < NV:
-                t_mx[r] = add("T", 0.23, [t_q[r // 4], t_wq], emit_mx(r, "qv", ct), due - 1000.0, take=("qv", ct))
+                t_mx[r] = add(
+                    "T",
+                    0.23,
+                    [t_q[r // 4], t_wq] + ([t_mx[r - 1]] if r > 0 else []),
+                    emit_mx(r, "qv", ct),
+                    due - 5000.0,
+                    take=("qv", ct),
+                )
 
-                def emit_v(r=r, ct=ct):
-                    for j in range(W):
+                t_done[r] = []
+                for j in range(W):
+
+                    def emit_v(r=r, j=j, ct=ct):
                         nc.vector.scalar_tensor_tensor(
                             out=v_junk[j][:],
                             in0=tiles["qv"][ct["qv"]][:],
@@ -296,27 +377,49 @@ def tile_crosssliceattention_pa_t_kernel(tc, x, Wq, bq, k_proj, out):
                             accum_out=sc[:, r, j : j + 1],
                         )
 
-                t_done[r] = [add("V", T_V, [t_mx[r]] + rows, emit_v, due, give=("qv", ct))]
+                    t_done[r].append(
+                        add(
+                            "V",
+                            T_V / W,
+                            [t_mx[r]] + rows + t_done[r][-1:],
+                            emit_v,
+                            5000.0 + r + 0.1 * j,
+                            give=((("qv", ct),) if j == W - 1 else ()),
+                        )
+                    )
             else:
-                t_mx[r] = add("T", 0.23, [t_q[r // 4], t_wq], emit_mx(r, "qs", ct), due - 500.0, take=("qs", ct))
-                t_s = add("N", 0.0, [t_mx[r]], None, due - 500.0, take=("qsb", ct))
+                t_s = add("N", 0.0, [t_q[r // 4], t_wq] + prev_g, None, due - 3.0, take=("qsb", ct))
+                prev_g = [t_s]
+                t_mx[r] = add("T", 0.23, [t_s], emit_mx(r, "ps", ct), due - 3.0, take=("ps", ct))
 
                 def emit_e(ct=ct):
-                    nc.scalar.mul(out=tiles["qsb"][ct["qsb"]][:], in_=tiles["qs"][ct["qs"]][:], mul=SCALE)
+                    nc.scalar.mul(out=tiles["qsb"][ct["qsb"]][:], in_=tiles["ps"][ct["ps"]][:], mul=SCALE)
 
-                t_e = add("S", 0.46, [t_s], emit_e, due - 500.0, give=("qs", ct))
+                t_e = add("S", 0.46, [t_mx[r]], emit_e, due - 2.0, give=(("ps", ct),))
                 t_p = add("N", 0.0, [t_e], None, due, take=("prod", ct))
 
-                def emit_g(r=r, ct=ct):
-                    nc.gpsimd.tensor_tensor(
-                        out=tiles["prod"][ct["prod"]][:],
-                        in0=tiles["qsb"][ct["qsb"]][:].unsqueeze(1).to_broadcast([P, W, D]),
-                        in1=k_sb[:, r : r + W, :],
-                        op=ALU.mult,
-                    )
-
-                t_g = add("G", T_G, [t_p] + rows, emit_g, due, give=("qsb", ct))
                 sums = []
+                t_gs = {}
+                for j0, j1 in G_SPLIT:
+
+                    def emit_g(r=r, j0=j0, j1=j1, ct=ct):
+                        nc.gpsimd.tensor_tensor(
+                            out=tiles["prod"][ct["prod"]][:, j0:j1, :],
+                            in0=tiles["qsb"][ct["qsb"]][:].unsqueeze(1).to_broadcast([P, j1 - j0, D]),
+                            in1=k_sb[:, r + j0 : r + j1, :],
+                            op=ALU.mult,
+                        )
+
+                    t_g = add(
+                        "G",
+                        0.2 + 0.855 * (j1 - j0),
+                        [t_p] + rows,
+                        emit_g,
+                        due + 0.01 * j0,
+                        give=((("qsb", ct),) if j1 == W else ()),
+                    )
+                    for j in range(j0, j1):
+                        t_gs[j] = t_g
                 for j in range(W):
 
                     def emit_r(r=r, j=j, ct=ct):
@@ -327,26 +430,23 @@ def tile_crosssliceattention_pa_t_kernel(tc, x, Wq, bq, k_proj, out):
                             accum_out=sc[:, r, j : j + 1],
                         )
 
-                    sums.append(add("S", 0.53, [t_g], emit_r, due + T_G + 0.5 * j))
-                add("N", 0.0, sums, None, 0.0, give=("prod", ct))
+                    sums.append(add("S", 0.5, [t_gs[j]], emit_r, due + 1.0 + 1.05 * j))
+                add("N", 0.0, sums, None, 0.0, give=(("prod", ct),))
                 t_done[r] = sums
-        for g in range(R // 4):
-            add("N", 0.0, [t_mx[4 * g + i] for i in range(4)], None, 0.0, give=("codes", cx_q[g]))
-
         t_cm = []
         for i0 in range(0, HR, 2):
             ck = {}
-            due = 3000.0 + i0
+            due = 20.0 + 1.15 * i0
 
             def emit_kt(i0=i0, ck=ck):
-                kt = tiles["tp"][ck["tp"]][:].rearrange("p (i u t) -> p i u t", i=2, u=2)
+                kt = tiles["ps"][ck["ps"]][:].rearrange("p (i u t) -> p i u t", i=2, u=2)
                 for i in range(2):
                     for u in range(2):
                         nc.tensor.transpose(kt[:, i, u, :], k32[:, i0 + i, u * P : (u + 1) * P], ident[:])
 
             def emit_kc(ck=ck):
                 nc.scalar.copy(
-                    out=tiles["ktsb"][ck["ktsb"]][:].rearrange("p i u t -> p (i u t)"), in_=tiles["tp"][ck["tp"]][:]
+                    out=tiles["ktsb"][ck["ktsb"]][:].rearrange("p i u t -> p (i u t)"), in_=tiles["ps"][ck["ps"]][:]
                 )
 
             def emit_cm(i0=i0, ck=ck):
@@ -362,52 +462,276 @@ def tile_crosssliceattention_pa_t_kernel(tc, x, Wq, bq, k_proj, out):
                         )
 
             t_s = add("N", 0.0, key_row_loads(i0, i0 + 2) + [t_ident], None, due, take=("ktsb", ck))
-            t_t = add("T", 0.45, [t_s], emit_kt, due, take=("tp", ck))
-            t_c = add("S", 0.46, [t_t], emit_kc, due, give=("tp", ck))
-            t_cm.append(add("T", 0.5, [t_c, t_b], emit_cm, due, give=("ktsb", ck)))
-        t_csb = add("S", 0.15, t_cm, lambda: nc.scalar.mul(out=c_sb[:], in_=c_ps[:, 0:HR], mul=SCALE), -1000.0)
+            t_t = add("T", 0.45, [t_s], emit_kt, due, take=("ps", ck))
+            t_c = add("S", 0.46, [t_t], emit_kc, due, give=(("ps", ck),))
+            t_cm.append(add("T", 0.5, [t_c, t_b], emit_cm, due, give=(("ktsb", ck),)))
+        t_csb = add(
+            "S",
+            0.15,
+            t_cm,
+            lambda: nc.scalar.mul(out=c_sb[:], in_=c_ps, mul=SCALE),
+            -5000.0,
+        )
 
-        def softmax(r0, r1, due):
+        def emit_cm_all():
+            for j in range(W):
+                nc.gpsimd.tensor_tensor(out=cm[:, :, j], in0=c_sb[:, j : j + R], in1=mask[:, :, j], op=ALU.add)
+
+        t_cmall = add("G", 1.3, [t_csb, t_mask], emit_cm_all, -5000.0)
+
+        def softmax(r0, r1, helper):
             n = r1 - r0
             cs = {}
-            deps = [t_csb, t_flags]
+            deps = [t_cmall]
             for r in range(r0, r1):
                 deps.extend(t_done[r])
+            eng = nc.gpsimd if helper == "G" else nc.vector
+            cost = 0.32 if helper == "G" else 0.15
 
-            def emit_a():
-                t1 = tiles["soft"][cs["soft"]][:, 0, 0:n, :]
-                mx = stats[cs["soft"]][:, 0, 0:n]
-                for j in range(W):
-                    nc.vector.tensor_tensor(out=t1[:, :, j], in0=sc[:, r0:r1, j], in1=c_sb[:, r0 + j : r1 + j], op=ALU.add)
-                for r, j0, j1, flag in ((0, 0, 2, f_lo), (1, 0, 1, f_lo), (R - 2, 4, 5, f_hi), (R - 1, 3, 5, f_hi)):
-                    if r0 <= r < r1:
-                        nc.vector.tensor_scalar_add(
-                            out=t1[:, r - r0, j0:j1], in0=t1[:, r - r0, j0:j1], scalar1=flag[:, 0:1]
-                        )
-                nc.vector.tensor_reduce(out=mx, in_=t1, axis=AX.X, op=ALU.max)
-                nc.vector.tensor_tensor(out=t1, in0=t1, in1=mx.unsqueeze(2).to_broadcast([P, n, W]), op=ALU.subtract)
+            def t1_of():
+                return tiles["soft"][cs["soft"]][:, 0, 0:n, :]
 
-            def emit_e():
-                both = tiles["soft"][cs["soft"]]
-                nc.scalar.activation(out=both[:, 1, 0:n, :], in_=both[:, 0, 0:n, :], func=ACT.Exp)
+            def ex_of():
+                return tiles["soft"][cs["soft"]][:, 1, 0:n, :]
 
-            def emit_n():
-                ex = tiles["soft"][cs["soft"]][:, 1, 0:n, :]
-                sm = stats[cs["soft"]][:, 1, 0:n]
-                nc.vector.tensor_reduce(out=sm, in_=ex, axis=AX.X, op=ALU.add)
-                nc.vector.reciprocal(out=sm, in_=sm)
-                nc.vector.tensor_tensor(
-                    out=out_sb[:, r0:r1, :], in0=ex, in1=sm.unsqueeze(2).to_broadcast([P, n, W]), op=ALU.mult
+            def st_of(i):
+                return stats[cs["soft"]][:, i, 0:n]
+
+            def emit_1():
+                eng.tensor_tensor(out=t1_of(), in0=sc[:, r0:r1, 0:W], in1=cm[:, r0:r1, :], op=ALU.add)
+
+            def emit_2():
+                nc.vector.tensor_reduce(out=st_of(0), in_=t1_of(), axis=AX.X, op=ALU.max)
+
+            def emit_3():
+                eng.tensor_tensor(
+                    out=t1_of(), in0=t1_of(), in1=st_of(0).unsqueeze(2).to_broadcast([P, n, W]), op=ALU.subtract
                 )
 
-            t_a = add("V", 0.9, deps, emit_a, -500.0, take=("soft", cs))
-            t_e = add("S", 0.2, [t_a], emit_e, -1000.0)
-            t_n = add("V", 0.4, [t_e], emit_n, -500.0, give=("soft", cs))
-            add("D", 0.2, [t_n], lambda: nc.sync.dma_start(out=out_v[:, r0:r1, :], in_=out_sb[:, r0:r1, :]), due)
+            def emit_4():
+                nc.scalar.activation(out=ex_of(), in_=t1_of(), func=ACT.Exp)
 
-        for r0, r1 in V_CHUNKS:
-            softmax(r0, r1, max(50.0, due_tile(r1 - 1) + T_V))
-        for r0, r1 in G_CHUNKS:
-            softmax(r0, r1, max(50.0, due_tile(r0) + 2 * T_G))
+            def emit_5():
+                nc.vector.tensor_reduce(out=st_of(1), in_=ex_of(), axis=AX.X, op=ALU.add)
+                nc.vector.reciprocal(out=st_of(1), in_=st_of(1))
+
+            def emit_6():
+                eng.tensor_tensor(
+                    out=out_sb[:, r0:r1, :], in0=ex_of(), in1=st_of(1).unsqueeze(2).to_broadcast([P, n, W]), op=ALU.mult
+                )
+
+            t = add(helper, cost, deps, emit_1, -500.0, take=("soft", cs))
+            t = add("V", 0.15, [t], emit_2, -500.0)
+            t = add(helper, cost, [t], emit_3, -500.0)
+            t = add("S", 0.2, [t], emit_4, -5000.0)
+            t = add("V", 0.3, [t], emit_5, -500.0)
+            t = add(helper, cost, [t], emit_6, -500.0, give=(("soft", cs),))
+            add("D", 0.2, [t], load(out_v[:, r0:r1, :], out_sb[:, r0:r1, :]), 0.0)
+
+        for r0, r1 in V_CHUNKS + G_CHUNKS:
+            softmax(r0, r1, "V" if r1 == NV else "G")
+
+        def emit_bias_t(cb):
+            def emit():
+                nc.tensor.transpose(tiles["ps"][cb["ps"]][:].bitcast(BF16)[:, 0:P], b_rows[:], ident_bf[:])
+
+            return emit
+
+        cb = {}
+        t_bt = add("T", 0.1, [t_b, t_masks], emit_bias_t(cb), -8000.0, take=("ps", cb))
+        t_bn = add(
+            "S",
+            0.1,
+            [t_bt],
+            lambda: nc.scalar.mul(out=b_nat[:], in_=tiles["ps"][cb["ps"]][:].bitcast(BF16)[:, 0:4], mul=SCALE),
+            -8000.0,
+            give=(("ps", cb),),
+        )
+
+        t_ext = []
+        prev_k = []
+        prev_q = []
+        for pi in range(NPAIR):
+            a = 8.0 + PACE_P * pi
+            cp = {}
+            b0 = T_BATCHES[2 * pi]
+            e = R // 4 + pi
+
+            def emit_lk(cp=cp, b0=b0):
+                nc.sync.dma_start(
+                    out=tiles["kb"][cp["kb"]][:], in_=k_proj[b0 : b0 + 2].rearrange("b (h p) d -> p (b h) d", p=P)
+                )
+
+            t_lk = add("N", 2.0, [add("D", 1.0, [], emit_lk, a - 4.0, take=("kb", cp))], None, 0.0)
+
+            t_kc = []
+            t_kts = []
+            cks = []
+            for be in range(2):
+                ck = {}
+                cks.append(ck)
+
+                def emit_kt2(be=be, ck=ck, cp=cp):
+                    ktb = tiles["ps"][ck["ps"]][:].bitcast(BF16).rearrange("p (c t) -> p c t", c=4)
+                    for h in range(2):
+                        for c in range(4):
+                            nc.tensor.transpose(
+                                ktb[:, c, h * P : (h + 1) * P],
+                                tiles["kb"][cp["kb"]][:, 2 * be + h, c * P : (c + 1) * P],
+                                ident_bf[:],
+                            )
+
+                def emit_kc2(ck=ck):
+                    ktb = tiles["ps"][ck["ps"]][:].bitcast(BF16).rearrange("p (c t) -> p c t", c=4)
+                    nc.scalar.copy(out=tiles["kT"][ck["kT"]][:, :, NB : NB + S], in_=ktb)
+
+                t_s = add("N", 0.0, [t_lk, t_masks, t_zero] + prev_k, None, a + 2.0 + 2.0 * be, take=("kT", ck))
+                prev_k = [t_s]
+                t_kts.append(add("T", 0.5, [t_s], emit_kt2, a + 2.0 + 2.0 * be, take=("ps", ck)))
+                t_kc.append(add("S", 0.9, [t_kts[be]], emit_kc2, a + 2.0 + 2.0 * be, give=(("ps", ck),)))
+            add("N", 0.0, t_kts, None, 0.0, give=(("kb", cp),))
+
+            t_s = add("N", 0.0, [t_qp[pi], t_wq] + prev_q, None, a + 5.0, take=("qT", cp))
+            prev_q = [t_s]
+            t_mts = []
+            t_qe = []
+            for c in range(4):
+                cc = {}
+
+                def emit_mt(c=c, cc=cc, e=e):
+                    nc.tensor.matmul_mx(
+                        out=tiles["ps"][cc["ps"]][:],
+                        lhsT=w_codes[:, c * P : (c + 1) * P].bitcast(FP8X4),
+                        lhsT_scale=w_scales[:, c * P : (c + 1) * P],
+                        rhs=codes_all[:, e, :].bitcast(FP8X4),
+                        rhs_scale=planes_all[:, e, :],
+                        start=True,
+                        stop=True,
+                    )
+
+                def emit_qe(c=c, cc=cc, cp=cp):
+                    nc.scalar.activation(
+                        out=tiles["qT"][cp["qT"]][:, c, :],
+                        in_=tiles["ps"][cc["ps"]][:],
+                        func=ACT.Identity,
+                        bias=b_nat[:, c : c + 1],
+                        scale=SCALE,
+                    )
+
+                t_mts.append(add("T", 0.23, [t_s], emit_mt, a + 5.0 + 0.5 * c, take=("ps", cc)))
+                t_qe.append(add("S", 0.5, [t_mts[c], t_bn], emit_qe, a + 5.0 + 0.5 * c, give=(("ps", cc),)))
+
+            t_bands = []
+            for be in range(2):
+                ce = {}
+                ck = cks[be]
+                tau = 4 * pi + 2 * be
+
+                def emit_bd(be=be, ce=ce, ck=ck, cp=cp):
+                    for h in range(2):
+                        for c in range(4):
+                            nc.tensor.matmul(
+                                out=tiles["sps"][ce["sps"]][:, h * BW : (h + 1) * BW],
+                                lhsT=tiles["qT"][cp["qT"]][:, c, (2 * be + h) * P : (2 * be + h + 1) * P],
+                                rhs=tiles["kT"][ck["kT"]][:, c, h * P : h * P + BW],
+                                start=(c == 0),
+                                stop=(c == 3),
+                            )
+
+                def emit_e1(ce=ce):
+                    nc.vector.tensor_tensor(
+                        out=tiles["mk"][ce["mk"]][:, :, 0:BW],
+                        in0=tiles["sps"][ce["sps"]][:, 0 : 2 * BW].rearrange("p (t n) -> p t n", t=2),
+                        in1=band01[:].unsqueeze(1).to_broadcast([P, 2, BW]),
+                        op=ALU.mult,
+                    )
+
+                def emit_e2(ce=ce, tau=tau):
+                    nc.vector.tensor_reduce(
+                        out=er2[:, tau : tau + 2, 0:W],
+                        in_=tiles["mk"][ce["mk"]][:].rearrange("p t (a m) -> p t m a", m=W),
+                        axis=AX.X,
+                        op=ALU.add,
+                    )
+
+                due = a + 8.0 + 2.0 * be
+                t_bd = add("T", 1.9, t_qe + [t_kc[be]], emit_bd, due, take=("sps", ce), give=(("kT", ck),))
+                t_bands.append(t_bd)
+                t_m = add("N", 0.0, [t_bd, t_band, t_zero], None, due, take=("mk", ce))
+                t_e1 = add("V", 0.3, [t_m], emit_e1, due, give=(("sps", ce),))
+                t_ext.append(add("V", 0.3, [t_e1], emit_e2, due + 1.0, give=(("mk", ce),)))
+            add("N", 0.0, t_bands, None, 0.0, give=(("qT", cp),))
+
+        def emit_f1():
+            nc.vector.tensor_copy(out=er2[:, :, W : 2 * W], in_=er2[:, :, 0:W])
+            nc.vector.tensor_scalar_mul(out=e_t[:], in0=er2[:, :, 0:W], scalar1=sel[:, 0:1])
+            for m in range(1, W):
+                nc.vector.scalar_tensor_tensor(
+                    out=e_t[:], in0=er2[:, :, m : m + W], scalar=sel[:, m : m + 1], in1=e_t[:], op0=ALU.mult, op1=ALU.add
+                )
+            e_v = e_t[:].rearrange("p (b h) j -> p b (h j)", h=2)
+            nc.vector.tensor_tensor(
+                out=e_v,
+                in0=e_v,
+                in1=mask_t[:].rearrange("p h j -> p (h j)").unsqueeze(1).to_broadcast([P, NTT // 2, 2 * W]),
+                op=ALU.add,
+            )
+            nc.vector.tensor_reduce(out=st_t[:, 0, :], in_=e_t[:], axis=AX.X, op=ALU.max)
+            nc.vector.tensor_tensor(
+                out=e_t[:], in0=e_t[:], in1=st_t[:, 0, :].unsqueeze(2).to_broadcast([P, NTT, W]), op=ALU.subtract
+            )
+
+        def emit_f3():
+            nc.vector.tensor_reduce(out=st_t[:, 1, :], in_=x_t[:], axis=AX.X, op=ALU.add)
+            nc.vector.reciprocal(out=st_t[:, 1, :], in_=st_t[:, 1, :])
+            nc.vector.tensor_tensor(
+                out=p_t[:, :, 0 : W * NTT // 2].rearrange("p g (t j) -> p g t j", j=W),
+                in0=x_t[:].rearrange("p (g t) j -> p g t j", g=2),
+                in1=st_t[:, 1, :].rearrange("p (g t) -> p g t", g=2).unsqueeze(3).to_broadcast([P, 2, NTT // 2, W]),
+                op=ALU.mult,
+            )
+
+        cf = {}
+        cg = {}
+
+        def emit_f4():
+            for g in range(2):
+                nc.tensor.transpose(tiles["ps"][cf["ps"]][:, g * P : (g + 1) * P], p_t[:, g, :], ident[:])
+
+        def emit_f6():
+            for e in range(2):
+                nc.tensor.transpose(tiles["ps"][cg["ps"]][:, e * P : (e + 1) * P], t1_sb[:, e : 2 * P : 2], ident[:])
+
+        def emit_f7():
+            nc.scalar.copy(
+                out=f_sb[:],
+                in_=tiles["ps"][cg["ps"]][:, 0 : 2 * P]
+                .rearrange("p (e c) -> p e c", e=2)[:, :, 0 : W * NTT // 2]
+                .rearrange("p e (t j) -> p t e j", j=W),
+            )
+
+        def emit_f8():
+            for g in range(2):
+                t0 = T_RANGES[g][0] * S
+                nc.sync.dma_start(
+                    out=out_f[t0 : t0 + NTT // 2 * P, :].rearrange("(t u e) j -> u t (e j)", t=NTT // 2, e=2),
+                    in_=f_sb[g * 64 : (g + 1) * 64].rearrange("u t e j -> u t (e j)"),
+                )
+
+        t_f1 = add("V", 1.8, t_ext + [t_masks], emit_f1, -400.0)
+        t_f2 = add("S", 0.25, [t_f1], lambda: nc.scalar.activation(out=x_t[:], in_=e_t[:], func=ACT.Exp), -5000.0)
+        t_f3 = add("V", 0.6, [t_f2, t_zero], emit_f3, -400.0)
+        t_f4 = add("T", 0.2, [t_f3], emit_f4, -400.0, take=("ps", cf))
+        t_f5 = add(
+            "S",
+            0.3,
+            [t_f4],
+            lambda: nc.scalar.copy(out=t1_sb[:], in_=tiles["ps"][cf["ps"]][:, 0 : 2 * P]),
+            -5000.0,
+            give=(("ps", cf),),
+        )
+        t_f6 = add("T", 0.25, [t_f5], emit_f6, -400.0, take=("ps", cg))
+        t_f7 = add("S", 0.25, [t_f6], emit_f7, -5000.0, give=(("ps", cg),))
+        add("D", 0.4, [t_f7], emit_f8, 0.0)
 
         run_schedule(tasks, slots)

@@ -43,7 +43,10 @@ G_START = 22.0
 PACE_G = 5.3
 PACE_P = 10.5
 NX = R // 4 + NPAIR
+G_FIX = 0.4
 LAT = 0.3
+C_START = 14.0
+C_PACE = 1.0
 LOG = []
 
 FLOPS = 2 * B * S * D * D + 2 * B * S * W * D
@@ -191,14 +194,15 @@ def tile_crosssliceattention_pa_t_kernel(tc, x, Wq, bq, k_proj, out):
 
         t_band = add("G", 2.0, [t_ident], emit_band, -8800.0)
 
-        def emit_zero_g():
+        def emit_zero():
             for t in tiles["kT"]:
-                nc.gpsimd.memset(t[:], 0.0)
+                nc.vector.memset(t[:, :, 0:NB], 0.0)
+                nc.vector.memset(t[:, :, NB + S : 2 * NB + S], 0.0)
             for t in tiles["mk"]:
-                nc.gpsimd.memset(t[:], 0.0)
-            nc.gpsimd.memset(p_t[:], 0.0)
+                nc.vector.memset(t[:, :, BW : BW + 3], 0.0)
+            nc.vector.memset(p_t[:], 0.0)
 
-        t_zero = add("G", 4.0, [], emit_zero_g, -8700.0)
+        t_zero = add("V", 0.9, [], emit_zero, -8950.0)
 
         def emit_consts_v():
             nc.vector.memset(b_rows[:], 0.0)
@@ -412,7 +416,7 @@ def tile_crosssliceattention_pa_t_kernel(tc, x, Wq, bq, k_proj, out):
 
                     t_g = add(
                         "G",
-                        0.2 + 0.855 * (j1 - j0),
+                        G_FIX + 0.855 * (j1 - j0),
                         [t_p] + rows,
                         emit_g,
                         due + 0.01 * j0,
@@ -436,7 +440,7 @@ def tile_crosssliceattention_pa_t_kernel(tc, x, Wq, bq, k_proj, out):
         t_cm = []
         for i0 in range(0, HR, 2):
             ck = {}
-            due = 20.0 + 1.15 * i0
+            due = C_START + C_PACE * i0
 
             def emit_kt(i0=i0, ck=ck):
                 kt = tiles["ps"][ck["ps"]][:].rearrange("p (i u t) -> p i u t", i=2, u=2)
@@ -475,9 +479,9 @@ def tile_crosssliceattention_pa_t_kernel(tc, x, Wq, bq, k_proj, out):
 
         def emit_cm_all():
             for j in range(W):
-                nc.gpsimd.tensor_tensor(out=cm[:, :, j], in0=c_sb[:, j : j + R], in1=mask[:, :, j], op=ALU.add)
+                nc.vector.tensor_tensor(out=cm[:, :, j], in0=c_sb[:, j : j + R], in1=mask[:, :, j], op=ALU.add)
 
-        t_cmall = add("G", 1.3, [t_csb, t_mask], emit_cm_all, -5000.0)
+        t_cmall = add("V", 0.6, [t_csb, t_mask], emit_cm_all, -5000.0)
 
         def softmax(r0, r1, helper):
             n = r1 - r0
@@ -529,7 +533,7 @@ def tile_crosssliceattention_pa_t_kernel(tc, x, Wq, bq, k_proj, out):
             add("D", 0.2, [t], load(out_v[:, r0:r1, :], out_sb[:, r0:r1, :]), 0.0)
 
         for r0, r1 in V_CHUNKS + G_CHUNKS:
-            softmax(r0, r1, "V" if r1 == NV else "G")
+            softmax(r0, r1, "V")
 
         def emit_bias_t(cb):
             def emit():

@@ -31,23 +31,30 @@ R = V_NB * S // P
 HR = R + 2 * NB
 TOK0 = V_B0 * S
 NTOK = V_NB * S
-NG = 10
+NG = 13
 NV = R - NG
 V_CHUNKS = ((0, 14), (14, NV - 2), (NV - 2, NV))
 G_CHUNKS = ((NV + 2, R), (NV, NV + 2))
 
-T_V = 2.35
+T_V = 2.9
 T_G = 5.25
-G_SPLIT = ((0, 1), (1, 2), (2, 3), (3, 4), (4, 5))
-G_START = 22.0
-PACE_G = 5.3
+G_SPLIT = ((0, 3), (3, 5))
+G_START = 10.0
+PACE_G = 5.0
 PACE_P = 10.5
 NX = R // 4 + NPAIR
-G_FIX = 0.4
+G_FIX = 0.3
 LAT = 0.3
 C_START = 14.0
 C_PACE = 1.0
 LOG = []
+BURSTS = (
+    ((("v", 0),), 0.0),
+    ((("v", 9), ("t", 0)), 1.0),
+    ((("t", 1), ("v", 1), ("v", 8), ("t", 2)), 12.0),
+    ((("v", 2), ("t", 3), ("v", 7), ("t", 4), ("v", 3)), 24.0),
+    ((("t", 5), ("v", 4), ("v", 6), ("v", 5)), 40.0),
+)
 
 FLOPS = 2 * B * S * D * D + 2 * B * S * W * D
 
@@ -134,7 +141,7 @@ def tile_crosssliceattention_pa_t_kernel(tc, x, Wq, bq, k_proj, out):
         mask = keep.tile([P, R, W], F32, name="mask")
         idx = keep.tile([P, R], I32, name="idx")
         loc = keep.tile([P, R], F32, name="loc")
-        out_sb = keep.tile([P, R, W], F32, name="out_sb")
+        out_sb = {"G": keep.tile([P, R, W], F32, name="out_g"), "V": keep.tile([P, R, W], F32, name="out_v")}
         band01 = keep.tile([P, BW], F32, name="band01")
         sel = keep.tile([P, W], F32, name="sel")
         mask_t = keep.tile([P, 2, W], F32, name="mask_t")
@@ -154,12 +161,12 @@ def tile_crosssliceattention_pa_t_kernel(tc, x, Wq, bq, k_proj, out):
             "ps": [banks[0], banks[1], banks[4], banks[5]],
             "qv": [banks[2], banks[3], banks[7]],
             "sps": banks[6:7],
-            "grp": many(3, [P, 4 * P, 4], BF16, "grp", 64),
+            "grp": many(5, [P, 4 * P, 4], BF16, "grp", 64),
             "ktsb": many(2, [P, 2, 2, P], F32, "ktsb"),
             "qsb": many(3, [P, D], F32, "qsb"),
             "prod": many(2, [P, W, D], F32, "prod"),
             "soft": many(2, [P, 2, 16, W], F32, "soft"),
-            "xs": many(6, [P, 4, D], BF16, "xs"),
+            "xs": many(5, [P, 4, D], BF16, "xs"),
             "kb": many(2, [P, 4, D], BF16, "kb"),
             "qT": many(2, [P, 4, 4 * P], F32, "qT"),
             "kT": many(3, [P, 4, S + 2 * NB], F32, "kT"),
@@ -232,7 +239,7 @@ def tile_crosssliceattention_pa_t_kernel(tc, x, Wq, bq, k_proj, out):
         t_mask = add("V", 0.7, [t_iota, t_cv0], emit_mask_v, -8800.0)
 
         def due_tile(r):
-            return 8.0 + T_V * 1.25 * r if r < NV else G_START + PACE_G * (R - 1 - r)
+            return 8.0 + T_V * 1.2 * r if r < NV else G_START + PACE_G * (R - 1 - r)
 
         t_w = add("D", 1.0, [], load(w_sb[:], Wq.rearrange("(c p) d -> p c d", p=P)), -9000.0)
         t_w = add("N", 2.0, [t_w], None, 0.0)
@@ -304,36 +311,45 @@ def tile_crosssliceattention_pa_t_kernel(tc, x, Wq, bq, k_proj, out):
         cxw, tsw, csw = quantise_four(lambda i: w32[:, i, :], [t_w], -9000.0, "V")
         t_wq = add("V", 0.47, csw, emit_quant(cxw, lambda: (w_codes[:], w_scales[:])), -9000.0, give=(("grp", cxw),))
 
-        def x_group(e, src, seq):
+        def x_group(e, src, seq, when):
             c0 = {}
-            t = add("D", 1.0, [], lambda: nc.sync.dma_start(out=tiles["xs"][c0["xs"]][:], in_=src), 0.5 * seq, take=("xs", c0))
+            t = add("D", 1.0, [], lambda: nc.sync.dma_start(out=tiles["xs"][c0["xs"]][:], in_=src), when - 8.0 + 0.1 * seq, take=("xs", c0))
             t = add("N", 2.0, [t], None, 0.0)
-            due = -7000.0 + seq
+            due = (when - 3.0) if when > 10.0 else (-7000.0 + seq)
             cx, t_ts, t_cs = quantise_four(lambda i: tiles["xs"][c0["xs"]][:].bitcast(F32)[:, i, :], [t], due, "S")
             add("N", 0.0, t_ts, None, 0.0, give=(("xs", c0),))
-            return add(
-                "V",
-                0.47,
-                t_cs,
-                emit_quant(cx, lambda: (codes_all[:, e, :], planes_all[:, e, :])),
-                due,
-                give=(("grp", cx),),
-            )
+            return cx, t_cs
 
-        order = []
-        for n in range(max(R // 4, NPAIR)):
-            if n < R // 4:
-                order.append(("v", n))
-            if n < NPAIR:
-                order.append(("t", n))
         t_q = {}
         t_qp = {}
-        for seq, (kind, n) in enumerate(order):
-            if kind == "v":
-                t_q[n] = x_group(n, x_v[:, 4 * n : 4 * n + 4, :], seq)
-            else:
-                b0 = T_BATCHES[2 * n]
-                t_qp[n] = x_group(R // 4 + n, x[b0 : b0 + 2].rearrange("b (h p) d -> p (b h) d", p=P), seq)
+        seq = 0
+        for burst, when in BURSTS:
+            deps = []
+            gives = []
+            emits = []
+            for kind, n in burst:
+                if kind == "v":
+                    e = n
+                    cx, t_cs = x_group(e, x_v[:, 4 * n : 4 * n + 4, :], seq, when)
+                else:
+                    e = R // 4 + n
+                    b0 = T_BATCHES[2 * n]
+                    cx, t_cs = x_group(e, x[b0 : b0 + 2].rearrange("b (h p) d -> p (b h) d", p=P), seq, when)
+                seq += 1
+                deps.extend(t_cs)
+                gives.append(("grp", cx))
+                emits.append(emit_quant(cx, lambda e=e: (codes_all[:, e, :], planes_all[:, e, :])))
+
+            def emit_burst(emits=emits):
+                for f in emits:
+                    f()
+
+            t = add("V", 0.47 * len(burst) + 0.4, deps, emit_burst, -7000.0 + seq, give=tuple(gives))
+            for kind, n in burst:
+                if kind == "v":
+                    t_q[n] = t
+                else:
+                    t_qp[n] = t
 
         def emit_mx(r, pool, ct):
             def emit():
@@ -479,9 +495,9 @@ def tile_crosssliceattention_pa_t_kernel(tc, x, Wq, bq, k_proj, out):
 
         def emit_cm_all():
             for j in range(W):
-                nc.vector.tensor_tensor(out=cm[:, :, j], in0=c_sb[:, j : j + R], in1=mask[:, :, j], op=ALU.add)
+                nc.gpsimd.tensor_tensor(out=cm[:, :, j], in0=c_sb[:, j : j + R], in1=mask[:, :, j], op=ALU.add)
 
-        t_cmall = add("V", 0.6, [t_csb, t_mask], emit_cm_all, -5000.0)
+        t_cmall = add("G", 1.3, [t_csb, t_mask], emit_cm_all, -5000.0)
 
         def softmax(r0, r1, helper):
             n = r1 - r0
@@ -521,7 +537,10 @@ def tile_crosssliceattention_pa_t_kernel(tc, x, Wq, bq, k_proj, out):
 
             def emit_6():
                 eng.tensor_tensor(
-                    out=out_sb[:, r0:r1, :], in0=ex_of(), in1=st_of(1).unsqueeze(2).to_broadcast([P, n, W]), op=ALU.mult
+                    out=out_sb[helper][:, r0:r1, :],
+                    in0=ex_of(),
+                    in1=st_of(1).unsqueeze(2).to_broadcast([P, n, W]),
+                    op=ALU.mult,
                 )
 
             t = add(helper, cost, deps, emit_1, -500.0, take=("soft", cs))
@@ -530,10 +549,10 @@ def tile_crosssliceattention_pa_t_kernel(tc, x, Wq, bq, k_proj, out):
             t = add("S", 0.2, [t], emit_4, -5000.0)
             t = add("V", 0.3, [t], emit_5, -500.0)
             t = add(helper, cost, [t], emit_6, -500.0, give=(("soft", cs),))
-            add("D", 0.2, [t], load(out_v[:, r0:r1, :], out_sb[:, r0:r1, :]), 0.0)
+            add("D", 0.2, [t], load(out_v[:, r0:r1, :], out_sb[helper][:, r0:r1, :]), 0.0)
 
         for r0, r1 in V_CHUNKS + G_CHUNKS:
-            softmax(r0, r1, "V")
+            softmax(r0, r1, "V" if r1 == NV else "G")
 
         def emit_bias_t(cb):
             def emit():

@@ -21,87 +21,28 @@ NB = 2
 SCALE = 1.0 / math.sqrt(D)
 NEG = -1.0e30
 
-T_RANGES = ((0, 6), (26, 32))
-T_BATCHES = tuple(range(0, 6)) + tuple(range(26, 32))
-NPAIR = len(T_BATCHES) // 2
-NTT = 2 * len(T_BATCHES)
+BAND_FIRST = (0, 26)
+BAND_BATCHES = 6
+PAIRS = BAND_BATCHES
+BAND_TILES = 4 * PAIRS
 BW = P + 2 * NB
-V_B0, V_NB = 6, 20
-R = V_NB * S // P
+R = 40
 HR = R + 2 * NB
-TOK0 = V_B0 * S
-NTOK = V_NB * S
-NG = 13
-NV = R - NG
-V_CHUNKS = ((0, 14), (14, NV - 2), (NV - 2, NV))
-G_CHUNKS = ((NV + 2, R), (NV, NV + 2))
-
-T_V = 2.9
-T_G = 5.25
-G_SPLIT = ((0, 3), (3, 5))
-G_START = 10.0
-PACE_G = 5.0
-PACE_P = 10.5
-NX = R // 4 + NPAIR
-G_FIX = 0.3
-LAT = 0.3
-C_START = 14.0
-C_PACE = 1.0
-LOG = []
-BURSTS = (
-    ((("v", 0),), 0.0),
-    ((("v", 9), ("t", 0)), 1.0),
-    ((("t", 1), ("v", 1), ("v", 8), ("t", 2)), 12.0),
-    ((("v", 2), ("t", 3), ("v", 7), ("t", 4), ("v", 3)), 24.0),
-    ((("t", 5), ("v", 4), ("v", 6), ("v", 5)), 40.0),
-)
+TOK0 = BAND_BATCHES * S
+NTOK = R * P
+NV = 28
+NG = R - NV
+GROUPS = R // 4 + PAIRS
+LAST_STEP = NV + 3
+SOFT_CHUNKS = ((24, 0, 12), (24, 12, 24), (NV + 1, NV, R), (NV, 24, NV))
+LATER_KEYS = (2, 3, 8, 4, 5, 7, 6)
 
 FLOPS = 2 * B * S * D * D + 2 * B * S * W * D
 
 
-def run_schedule(tasks, slots):
-    n = len(tasks)
-    fin = [-1.0] * n
-    busy = {"T": 0.0, "S": 0.0, "V": 0.0, "G": 0.0, "D": 0.0}
-    todo = list(range(n))
-    while todo:
-        best = None
-        for i in todo:
-            eng, dur, deps, emit, due, take, give = tasks[i]
-            est = busy.get(eng, 0.0)
-            ok = True
-            for d in deps:
-                if fin[d] < 0.0:
-                    ok = False
-                    break
-                est = max(est, fin[d] + (LAT if tasks[d][0] not in ("N", eng) else 0.0))
-            if not ok:
-                continue
-            if take is not None:
-                free = [f for f in slots[take[0]] if f >= 0.0]
-                if not free:
-                    continue
-                est = max(est, min(free))
-            key = (est, due, i)
-            if best is None or key < best:
-                best = key
-        assert best is not None
-        est, due, i = best
-        eng, dur, deps, emit, due, take, give = tasks[i]
-        if take is not None:
-            pool = slots[take[0]]
-            k = pool.index(min(f for f in pool if f >= 0.0))
-            pool[k] = -1.0
-            take[1][take[0]] = k
-        fin[i] = est + dur
-        if eng in busy:
-            busy[eng] = fin[i]
-        for g in give:
-            slots[g[0]][g[1][g[0]]] = fin[i] + LAT
-        if emit is not None:
-            emit()
-        LOG.append((eng, est, fin[i], i))
-        todo = [j for j in todo if j != i]
+def turn(t, first, period, count):
+    n, rest = divmod(t - first, period)
+    return n if rest == 0 and 0 <= n < count else None
 
 
 def tile_crosssliceattention_pa_t_kernel(tc, x, Wq, bq, k_proj, out):
@@ -109,652 +50,447 @@ def tile_crosssliceattention_pa_t_kernel(tc, x, Wq, bq, k_proj, out):
     x_f = x.flatten_outer_dims()
     k_f = k_proj.flatten_outer_dims()
     out_f = out.flatten_outer_dims()
-    x_v = x_f[TOK0 : TOK0 + NTOK, :].rearrange("(p r) d -> p r d", r=R)
-    k_lo = k_f[TOK0 - NB : TOK0 - NB + NTOK, :].rearrange("(p r) d -> p r d", r=R)
-    k_hi = k_f[TOK0 - NB + R : TOK0 - NB + R + NTOK, :].rearrange("(p r) d -> p r d", r=R)
-    out_v = out_f[TOK0 : TOK0 + NTOK, :].rearrange("(p r) j -> p r j", r=R)
+    x_rows = x_f[TOK0 : TOK0 + NTOK, :].rearrange("(p r) d -> p r d", r=R)
+    k_rows = k_f[TOK0 - NB : TOK0 - NB + NTOK, :].rearrange("(p r) d -> p r d", r=R)
+    k_tail = k_f[TOK0 - NB + R : TOK0 - NB + R + NTOK, :].rearrange("(p r) d -> p r d", r=R)
+    out_rows = out_f[TOK0 : TOK0 + NTOK, :].rearrange("(p r) j -> p r j", r=R)
 
     with ExitStack() as ctx:
-        keep = ctx.enter_context(tc.tile_pool(name="keep", bufs=1))
-        psum = ctx.enter_context(tc.psum_pool(name="psum", bufs=1))
+        fixed = ctx.enter_context(tc.tile_pool(name="fixed", bufs=1))
+        x_pool = ctx.enter_context(tc.tile_pool(name="x_pool", bufs=6))
+        stage = ctx.enter_context(tc.tile_pool(name="stage", bufs=3))
+        two = ctx.enter_context(tc.tile_pool(name="two", bufs=2))
+        scrap = ctx.enter_context(tc.tile_pool(name="scrap", bufs=4))
+        ps_short = ctx.enter_context(tc.psum_pool(name="ps_short", bufs=3))
+        ps_q = ctx.enter_context(tc.psum_pool(name="ps_q", bufs=3))
+        ps_fixed = ctx.enter_context(tc.psum_pool(name="ps_fixed", bufs=1))
         ctx.enter_context(tc.manual_schedule())
 
-        def many(n, shape, dtype, name, align=None):
-            if align is None:
-                return [keep.tile(shape, dtype, name="%s%d" % (name, i)) for i in range(n)]
-            return [keep.tile(shape, dtype, align_bytes=align, name="%s%d" % (name, i)) for i in range(n)]
+        ident = fixed.tile([P, P], F32, name="ident")
+        ident_bf = fixed.tile([P, P], BF16, name="ident_bf")
+        k_sb = fixed.tile([P, HR, D], BF16, name="k_sb")
+        w_sb = fixed.tile([P, 4, D], BF16, name="w_sb")
+        w_codes = fixed.tile([P, D], U32, align_bytes=64, name="w_codes")
+        w_scales = fixed.tile([P, D], U8, align_bytes=64, name="w_scales")
+        x_codes = fixed.tile([P, GROUPS, 4 * P], U32, align_bytes=64, name="x_codes")
+        x_scales = fixed.tile([P, GROUPS, 4 * P], U8, align_bytes=64, name="x_scales")
+        b_words = fixed.tile([P, 4], BF16, name="b_words")
+        b_rows = fixed.tile([P, P], BF16, name="b_rows")
+        b_part = fixed.tile([P, 4], F32, name="b_part")
+        score = fixed.tile([P, R, 8], F32, name="score")
+        c_sb = fixed.tile([P, HR], F32, name="c_sb")
+        c_mask = fixed.tile([P, R, W], F32, name="c_mask")
+        mask = fixed.tile([P, R, W], F32, name="mask")
+        place = fixed.tile([P, R], I32, name="place")
+        place_f = fixed.tile([P, R], F32, name="place_f")
+        out_sb = fixed.tile([P, R, W], F32, name="out_sb")
+        band01 = fixed.tile([P, BW], F32, name="band01")
+        turned = fixed.tile([P, W], F32, name="turned")
+        edge = fixed.tile([P, 2, W], F32, name="edge")
+        picked = fixed.tile([P, BAND_TILES, 2 * W], F32, name="picked")
+        band_s = fixed.tile([P, BAND_TILES, W], F32, name="band_s")
+        band_e = fixed.tile([P, BAND_TILES, W], F32, name="band_e")
+        band_m = fixed.tile([P, 2, BAND_TILES], F32, name="band_m")
+        band_p = fixed.tile([P, 2, P], F32, name="band_p")
+        band_t = fixed.tile([P, 2 * P], F32, name="band_t")
+        band_o = fixed.tile([P, BAND_TILES // 2, 2, W], F32, name="band_o")
+        keys_t = [fixed.tile([P, 4, S + 2 * NB], F32, name="keys_t%d" % i) for i in range(3)]
+        kept = [fixed.tile([P, 2, BW + 3], F32, name="kept%d" % i) for i in range(2)]
+        band_ps = ps_fixed.tile([P, 2 * BW], F32, name="band_ps")[:]
+        c_ps = ps_fixed.tile([P, HR], F32, name="c_ps")[:]
 
-        ident = keep.tile([P, P], F32, name="ident")
-        ident_bf = keep.tile([P, P], BF16, name="ident_bf")
-        codes_all = keep.tile([P, NX, 4 * P], U32, align_bytes=64, name="codes_all")
-        planes_all = keep.tile([P, NX, 4 * P], U8, align_bytes=64, name="planes_all")
-        k_sb = keep.tile([P, HR, D], BF16, name="k_sb")
-        w_sb = keep.tile([P, 4, D], BF16, name="w_sb")
-        b_cols = keep.tile([P, 4], BF16, name="b_cols")
-        b_rows = keep.tile([P, P], BF16, name="b_rows")
-        b_nat = keep.tile([P, 4], F32, name="b_nat")
-        w_codes = keep.tile([P, D], U32, align_bytes=64, name="w_codes")
-        w_scales = keep.tile([P, D], U8, align_bytes=64, name="w_scales")
-        sc = keep.tile([P, R, 8], F32, name="sc")
-        c_sb = keep.tile([P, HR], F32, name="c_sb")
-        cm = keep.tile([P, R, W], F32, name="cm")
-        mask = keep.tile([P, R, W], F32, name="mask")
-        idx = keep.tile([P, R], I32, name="idx")
-        loc = keep.tile([P, R], F32, name="loc")
-        out_sb = {"G": keep.tile([P, R, W], F32, name="out_g"), "V": keep.tile([P, R, W], F32, name="out_v")}
-        band01 = keep.tile([P, BW], F32, name="band01")
-        sel = keep.tile([P, W], F32, name="sel")
-        mask_t = keep.tile([P, 2, W], F32, name="mask_t")
-        er2 = keep.tile([P, NTT, 2 * W], F32, name="er2")
-        e_t = keep.tile([P, NTT, W], F32, name="e_t")
-        x_t = keep.tile([P, NTT, W], F32, name="x_t")
-        st_t = keep.tile([P, 2, NTT], F32, name="st_t")
-        p_t = keep.tile([P, 2, P], F32, name="p_t")
-        t1_sb = keep.tile([P, 2 * P], F32, name="t1_sb")
-        f_sb = keep.tile([P, NTT // 2, 2, W], F32, name="f_sb")
-        v_junk = many(5, [P, D], F32, "v_junk")
-        s_junk = many(5, [P, D], BF16, "s_junk")
-        banks = [psum.tile([P, 512], F32, name="bank%d" % i) for i in range(8)]
-        c_ps = banks[6][:, 2 * BW : 2 * BW + HR]
+        k_words = k_sb[:].bitcast(F32)
+        x_in, grouped, q_ps, prod, kb_in, kt_sb, q_t, soft = {}, {}, {}, {}, {}, {}, {}, {}
 
-        tiles = {
-            "ps": [banks[0], banks[1], banks[4], banks[5]],
-            "qv": [banks[2], banks[3], banks[7]],
-            "sps": banks[6:7],
-            "grp": many(5, [P, 4 * P, 4], BF16, "grp", 64),
-            "ktsb": many(2, [P, 2, 2, P], F32, "ktsb"),
-            "qsb": many(3, [P, D], F32, "qsb"),
-            "prod": many(2, [P, W, D], F32, "prod"),
-            "soft": many(2, [P, 2, 16, W], F32, "soft"),
-            "xs": many(5, [P, 4, D], BF16, "xs"),
-            "kb": many(2, [P, 4, D], BF16, "kb"),
-            "qT": many(2, [P, 4, 4 * P], F32, "qT"),
-            "kT": many(3, [P, 4, S + 2 * NB], F32, "kT"),
-            "mk": many(2, [P, 2, BW + 3], F32, "mk"),
-        }
-        stats = many(2, [P, 2, 16], F32, "stats")
-        slots = {}
-        for name in tiles:
-            slots[name] = [0.0] * len(tiles[name])
+        def load_keys(g):
+            src = k_rows[:, 4 * g : 4 * g + 4, :] if g < R // 4 else k_tail[:, 0:4, :]
+            nc.sync.dma_start(out=k_sb[:, 4 * g : 4 * g + 4, :], in_=src)
 
-        w32 = w_sb[:].bitcast(F32)
-        k32 = k_sb[:].bitcast(F32)
+        def pair_batch(pi):
+            return BAND_FIRST[pi // 3] + 2 * (pi % 3)
 
-        tasks = []
-
-        def add(eng, dur, deps, emit, due, take=None, give=()):
-            tasks.append([eng, dur, deps, emit, due, take, give])
-            return len(tasks) - 1
-
-        def load(out_ap, in_ap):
-            return lambda: nc.sync.dma_start(out=out_ap, in_=in_ap)
-
-        t_ident = add("G", 1.0, [], lambda: make_identity(nc, ident[:]), -9000.0)
-        t_iota = add(
-            "G", 0.3, [], lambda: nc.gpsimd.iota(idx[:], pattern=[[1, R]], base=0, channel_multiplier=R), -8900.0
-        )
-
-        def emit_band():
-            nc.gpsimd.memset(band01[:], 0.0)
-            for j in range(W):
-                nc.gpsimd.tensor_tensor(out=band01[:, j : j + P], in0=band01[:, j : j + P], in1=ident[:], op=ALU.add)
-
-        t_band = add("G", 2.0, [t_ident], emit_band, -8800.0)
-
-        def emit_zero():
-            for t in tiles["kT"]:
-                nc.vector.memset(t[:, :, 0:NB], 0.0)
-                nc.vector.memset(t[:, :, NB + S : 2 * NB + S], 0.0)
-            for t in tiles["mk"]:
-                nc.vector.memset(t[:, :, BW : BW + 3], 0.0)
-            nc.vector.memset(p_t[:], 0.0)
-
-        t_zero = add("V", 0.9, [], emit_zero, -8950.0)
-
-        def emit_consts_v():
-            nc.vector.memset(b_rows[:], 0.0)
-            nc.vector.memset(mask[:], 0.0)
-            nc.vector.memset(mask_t[:], 0.0)
-
-        t_cv0 = add("V", 0.4, [], emit_consts_v, -9000.0)
-
-        def emit_masks():
-            nc.vector.tensor_copy(out=ident_bf[:], in_=ident[:])
-            for m in range(W):
-                nc.vector.tensor_reduce(out=sel[:, m : m + 1], in_=ident[:, m:P:W], axis=AX.X, op=ALU.add)
-            nc.vector.tensor_reduce(out=mask_t[:, 0, 0:1], in_=ident[:, 0:2], axis=AX.X, op=ALU.add)
-            nc.vector.tensor_copy(out=mask_t[:, 0, 1:2], in_=ident[:, 0:1])
-            nc.vector.tensor_copy(out=mask_t[:, 1, 3:4], in_=ident[:, P - 1 : P])
-            nc.vector.tensor_reduce(out=mask_t[:, 1, 4:5], in_=ident[:, P - 2 : P], axis=AX.X, op=ALU.add)
-            nc.vector.tensor_scalar_mul(out=mask_t[:], in0=mask_t[:], scalar1=NEG)
-
-        t_masks = add("V", 1.2, [t_ident, t_cv0], emit_masks, -8900.0)
-
-        def emit_mask_v():
-            nc.vector.tensor_single_scalar(out=idx[:], in_=idx[:], scalar=S - 1, op=ALU.bitwise_and)
-            nc.vector.tensor_copy(out=loc[:], in_=idx[:])
-            for j, op, lim in ((0, ALU.is_lt, 2.0), (1, ALU.is_lt, 1.0), (3, ALU.is_gt, S - 2.0), (4, ALU.is_gt, S - 3.0)):
-                nc.vector.tensor_scalar(out=mask[:, :, j], in0=loc[:], scalar1=lim, scalar2=NEG, op0=op, op1=ALU.mult)
-
-        t_mask = add("V", 0.7, [t_iota, t_cv0], emit_mask_v, -8800.0)
-
-        def due_tile(r):
-            return 8.0 + T_V * 1.2 * r if r < NV else G_START + PACE_G * (R - 1 - r)
-
-        t_w = add("D", 1.0, [], load(w_sb[:], Wq.rearrange("(c p) d -> p c d", p=P)), -9000.0)
-        t_w = add("N", 2.0, [t_w], None, 0.0)
-
-        def emit_bias_load():
-            with nc.allow_non_contiguous_dma(reason="bias, two neighbouring values to a partition"):
-                nc.scalar.dma_start(
-                    out=b_cols[:].rearrange("w (u e) -> w u e", e=2),
-                    in_=bq.rearrange("(u w e) -> w u e", u=2, e=2),
-                )
-            nc.scalar.dma_start(out=b_rows[0:4, :], in_=bq.rearrange("(c p) -> c p", p=P))
-
-        t_b = add("S", 0.2, [t_cv0], emit_bias_load, -9000.0)
-        t_b = add("N", 4.0, [t_b], None, 0.0)
-
-        t_k = {}
-        for g in range(HR // 4):
-            near = min(due_tile(max(0, 4 * g - 4)), due_tile(min(R - 1, 4 * g + 3)))
-            src = k_lo[:, 4 * g : 4 * g + 4, :] if g < R // 4 else k_hi[:, 0:4, :]
-            t = add("D", 1.0, [], load(k_sb[:, 4 * g : 4 * g + 4, :], src), near - 6.0)
-            t_k[g] = add("N", 2.0, [t], None, 0.0)
-
-        def key_row_loads(i0, i1):
-            deps = []
-            for i in range(i0, i1):
-                if t_k[i // 4] not in deps:
-                    deps.append(t_k[i // 4])
-            return deps
-
-        def quantise_four(words_of, deps, due, copy_engine):
-            cx = {}
-            t_ts = []
-            t_cs = []
-            t_g = add("N", 0.0, deps, None, due, take=("grp", cx))
-            for h in range(2):
-                ch = {}
-
-                def emit_t(h=h, ch=ch):
-                    xt = tiles["ps"][ch["ps"]][:].rearrange("p (i u t) -> p i u t", i=2, u=2)
-                    for i in range(2):
-                        for u in range(2):
-                            nc.tensor.transpose(xt[:, i, u, :], words_of(2 * h + i)[:, u * P : (u + 1) * P], ident[:])
-
-                def emit_c(h=h, ch=ch):
-                    xt = tiles["ps"][ch["ps"]][:].rearrange("p (i u t) -> p i u t", i=2, u=2)
-                    g32 = tiles["grp"][cx["grp"]][:].bitcast(F32)
-                    dst = g32[:, 2 * h * P : (2 * h + 2) * P, :].rearrange("p (i t) u -> p i t u", i=2)
-                    src = xt.rearrange("p i u t -> p i t u")
-                    if copy_engine == "V":
-                        nc.vector.tensor_copy(out=dst, in_=src)
-                    else:
-                        nc.scalar.copy(out=dst, in_=src)
-
-                t_ts.append(add("T", 0.45, [t_ident, t_g], emit_t, due, take=("ps", ch)))
-                t_cs.append(add(copy_engine, 0.46, [t_ts[h]], emit_c, due, give=(("ps", ch),)))
-            return cx, t_ts, t_cs
-
-        def emit_quant(cx, codes_of):
-            def emit():
-                codes, scales = codes_of()
-                nc.vector.quantize_mx(
-                    out=codes.bitcast(FP8X4),
-                    scales=scales,
-                    in_=tiles["grp"][cx["grp"]][:].rearrange("p t j -> p (t j)"),
-                )
-
-            return emit
-
-        cxw, tsw, csw = quantise_four(lambda i: w32[:, i, :], [t_w], -9000.0, "V")
-        t_wq = add("V", 0.47, csw, emit_quant(cxw, lambda: (w_codes[:], w_scales[:])), -9000.0, give=(("grp", cxw),))
-
-        def x_group(e, src, seq, when):
-            c0 = {}
-            t = add("D", 1.0, [], lambda: nc.sync.dma_start(out=tiles["xs"][c0["xs"]][:], in_=src), when - 8.0 + 0.1 * seq, take=("xs", c0))
-            t = add("N", 2.0, [t], None, 0.0)
-            due = (when - 3.0) if when > 10.0 else (-7000.0 + seq)
-            cx, t_ts, t_cs = quantise_four(lambda i: tiles["xs"][c0["xs"]][:].bitcast(F32)[:, i, :], [t], due, "S")
-            add("N", 0.0, t_ts, None, 0.0, give=(("xs", c0),))
-            return cx, t_cs
-
-        t_q = {}
-        t_qp = {}
-        seq = 0
-        for burst, when in BURSTS:
-            deps = []
-            gives = []
-            emits = []
-            for kind, n in burst:
-                if kind == "v":
-                    e = n
-                    cx, t_cs = x_group(e, x_v[:, 4 * n : 4 * n + 4, :], seq, when)
-                else:
-                    e = R // 4 + n
-                    b0 = T_BATCHES[2 * n]
-                    cx, t_cs = x_group(e, x[b0 : b0 + 2].rearrange("b (h p) d -> p (b h) d", p=P), seq, when)
-                seq += 1
-                deps.extend(t_cs)
-                gives.append(("grp", cx))
-                emits.append(emit_quant(cx, lambda e=e: (codes_all[:, e, :], planes_all[:, e, :])))
-
-            def emit_burst(emits=emits):
-                for f in emits:
-                    f()
-
-            t = add("V", 0.47 * len(burst) + 0.4, deps, emit_burst, -7000.0 + seq, give=tuple(gives))
-            for kind, n in burst:
-                if kind == "v":
-                    t_q[n] = t
-                else:
-                    t_qp[n] = t
-
-        def emit_mx(r, pool, ct):
-            def emit():
-                i = r % 4
-                nc.tensor.matmul_mx(
-                    out=tiles[pool][ct[pool]][:],
-                    lhsT=codes_all[:, r // 4, i * P : (i + 1) * P].bitcast(FP8X4),
-                    lhsT_scale=planes_all[:, r // 4, i * P : (i + 1) * P],
-                    rhs=w_codes[:].bitcast(FP8X4),
-                    rhs_scale=w_scales[:],
-                    start=True,
-                    stop=True,
-                )
-
-            return emit
-
-        t_mx = {}
-        t_done = {}
-        prev_g = []
-        for r in list(range(NV)) + list(range(R - 1, NV - 1, -1)):
-            ct = {}
-            due = due_tile(r)
-            rows = key_row_loads(r, r + W)
-            if r < NV:
-                t_mx[r] = add(
-                    "T",
-                    0.23,
-                    [t_q[r // 4], t_wq] + ([t_mx[r - 1]] if r > 0 else []),
-                    emit_mx(r, "qv", ct),
-                    due - 5000.0,
-                    take=("qv", ct),
-                )
-
-                t_done[r] = []
-                for j in range(W):
-
-                    def emit_v(r=r, j=j, ct=ct):
-                        nc.vector.scalar_tensor_tensor(
-                            out=v_junk[j][:],
-                            in0=tiles["qv"][ct["qv"]][:],
-                            scalar=SCALE,
-                            in1=k_sb[:, r + j, :],
-                            op0=ALU.mult,
-                            op1=ALU.mult,
-                            accum_out=sc[:, r, j : j + 1],
-                        )
-
-                    t_done[r].append(
-                        add(
-                            "V",
-                            T_V / W,
-                            [t_mx[r]] + rows + t_done[r][-1:],
-                            emit_v,
-                            5000.0 + r + 0.1 * j,
-                            give=((("qv", ct),) if j == W - 1 else ()),
-                        )
-                    )
+        def load_x(e):
+            x_in[e] = x_pool.tile([P, 4, D], BF16, name="x_in")
+            if e < R // 4:
+                src = x_rows[:, 4 * e : 4 * e + 4, :]
             else:
-                t_s = add("N", 0.0, [t_q[r // 4], t_wq] + prev_g, None, due - 3.0, take=("qsb", ct))
-                prev_g = [t_s]
-                t_mx[r] = add("T", 0.23, [t_s], emit_mx(r, "ps", ct), due - 3.0, take=("ps", ct))
+                b0 = pair_batch(e - R // 4)
+                src = x[b0 : b0 + 2].rearrange("b (h p) d -> p (b h) d", p=P)
+            nc.sync.dma_start(out=x_in[e][:], in_=src)
 
-                def emit_e(ct=ct):
-                    nc.scalar.mul(out=tiles["qsb"][ct["qsb"]][:], in_=tiles["ps"][ct["ps"]][:], mul=SCALE)
+        def load_band_keys(pi):
+            b0 = pair_batch(pi)
+            kb_in[pi] = two.tile([P, 4, D], BF16, name="kb_in")
+            nc.sync.dma_start(out=kb_in[pi][:], in_=k_proj[b0 : b0 + 2].rearrange("b (h p) d -> p (b h) d", p=P))
 
-                t_e = add("S", 0.46, [t_mx[r]], emit_e, due - 2.0, give=(("ps", ct),))
-                t_p = add("N", 0.0, [t_e], None, due, take=("prod", ct))
-
-                sums = []
-                t_gs = {}
-                for j0, j1 in G_SPLIT:
-
-                    def emit_g(r=r, j0=j0, j1=j1, ct=ct):
-                        nc.gpsimd.tensor_tensor(
-                            out=tiles["prod"][ct["prod"]][:, j0:j1, :],
-                            in0=tiles["qsb"][ct["qsb"]][:].unsqueeze(1).to_broadcast([P, j1 - j0, D]),
-                            in1=k_sb[:, r + j0 : r + j1, :],
-                            op=ALU.mult,
-                        )
-
-                    t_g = add(
-                        "G",
-                        G_FIX + 0.855 * (j1 - j0),
-                        [t_p] + rows,
-                        emit_g,
-                        due + 0.01 * j0,
-                        give=((("qsb", ct),) if j1 == W else ()),
-                    )
-                    for j in range(j0, j1):
-                        t_gs[j] = t_g
-                for j in range(W):
-
-                    def emit_r(r=r, j=j, ct=ct):
-                        nc.scalar.activation(
-                            out=s_junk[j][:],
-                            in_=tiles["prod"][ct["prod"]][:, j, :],
-                            func=ACT.Copy,
-                            accum_out=sc[:, r, j : j + 1],
-                        )
-
-                    sums.append(add("S", 0.5, [t_gs[j]], emit_r, due + 1.0 + 1.05 * j))
-                add("N", 0.0, sums, None, 0.0, give=(("prod", ct),))
-                t_done[r] = sums
-        t_cm = []
-        for i0 in range(0, HR, 2):
-            ck = {}
-            due = C_START + C_PACE * i0
-
-            def emit_kt(i0=i0, ck=ck):
-                kt = tiles["ps"][ck["ps"]][:].rearrange("p (i u t) -> p i u t", i=2, u=2)
+        def pack_four(words_of, copy):
+            packed = stage.tile([P, 4 * P, 4], BF16, align_bytes=64, name="packed")
+            packed_words = packed[:].bitcast(F32)
+            for h in range(2):
+                bank = ps_short.tile([P, 512], F32, name="bank")
+                halves = bank[:].rearrange("p (i u t) -> p i u t", i=2, u=2)
                 for i in range(2):
                     for u in range(2):
-                        nc.tensor.transpose(kt[:, i, u, :], k32[:, i0 + i, u * P : (u + 1) * P], ident[:])
-
-            def emit_kc(ck=ck):
-                nc.scalar.copy(
-                    out=tiles["ktsb"][ck["ktsb"]][:].rearrange("p i u t -> p (i u t)"), in_=tiles["ps"][ck["ps"]][:]
+                        nc.tensor.transpose(halves[:, i, u, :], words_of(2 * h + i)[:, u * P : (u + 1) * P], ident[:])
+                copy(
+                    out=packed_words[:, 2 * h * P : (2 * h + 2) * P, :].rearrange("p (i t) u -> p i t u", i=2),
+                    in_=halves.rearrange("p i u t -> p i t u"),
                 )
+            return packed
 
-            def emit_cm(i0=i0, ck=ck):
-                kt_bf = tiles["ktsb"][ck["ktsb"]][:].bitcast(BF16).rearrange("p i u (t e) -> p i u t e", e=2)
-                for i in range(2):
-                    for n in range(4):
-                        nc.tensor.matmul(
-                            out=c_ps[:, i0 + i : i0 + i + 1],
-                            lhsT=kt_bf[:, i, n // 2, :, n % 2],
-                            rhs=b_cols[:, n : n + 1],
-                            start=(n == 0),
-                            stop=(n == 3),
-                        )
+        def quantise(packed, codes, scales):
+            nc.vector.quantize_mx(out=codes.bitcast(FP8X4), scales=scales, in_=packed[:].rearrange("p t j -> p (t j)"))
 
-            t_s = add("N", 0.0, key_row_loads(i0, i0 + 2) + [t_ident], None, due, take=("ktsb", ck))
-            t_t = add("T", 0.45, [t_s], emit_kt, due, take=("ps", ck))
-            t_c = add("S", 0.46, [t_t], emit_kc, due, give=(("ps", ck),))
-            t_cm.append(add("T", 0.5, [t_c, t_b], emit_cm, due, give=(("ktsb", ck),)))
-        t_csb = add(
-            "S",
-            0.15,
-            t_cm,
-            lambda: nc.scalar.mul(out=c_sb[:], in_=c_ps, mul=SCALE),
-            -5000.0,
-        )
+        def stage_x(e):
+            grouped[e] = pack_four(lambda i: x_in[e][:].bitcast(F32)[:, i, :], nc.scalar.copy)
 
-        def emit_cm_all():
+        def quantise_x(e):
+            quantise(grouped[e], x_codes[:, e, :], x_scales[:, e, :])
+
+        def q_tokens(r, bank):
+            nc.tensor.matmul_mx(
+                out=bank[:],
+                lhsT=x_codes[:, r // 4, (r % 4) * P : (r % 4 + 1) * P].bitcast(FP8X4),
+                lhsT_scale=x_scales[:, r // 4, (r % 4) * P : (r % 4 + 1) * P],
+                rhs=w_codes[:].bitcast(FP8X4),
+                rhs_scale=w_scales[:],
+                start=True,
+                stop=True,
+            )
+
+        def vector_q(r):
+            q_ps[r] = ps_q.tile([P, D], F32, name="q_ps")
+            q_tokens(r, q_ps[r])
+
+        def vector_tile(r):
             for j in range(W):
-                nc.gpsimd.tensor_tensor(out=cm[:, :, j], in0=c_sb[:, j : j + R], in1=mask[:, :, j], op=ALU.add)
-
-        t_cmall = add("G", 1.3, [t_csb, t_mask], emit_cm_all, -5000.0)
-
-        def softmax(r0, r1, helper):
-            n = r1 - r0
-            cs = {}
-            deps = [t_cmall]
-            for r in range(r0, r1):
-                deps.extend(t_done[r])
-            eng = nc.gpsimd if helper == "G" else nc.vector
-            cost = 0.32 if helper == "G" else 0.15
-
-            def t1_of():
-                return tiles["soft"][cs["soft"]][:, 0, 0:n, :]
-
-            def ex_of():
-                return tiles["soft"][cs["soft"]][:, 1, 0:n, :]
-
-            def st_of(i):
-                return stats[cs["soft"]][:, i, 0:n]
-
-            def emit_1():
-                eng.tensor_tensor(out=t1_of(), in0=sc[:, r0:r1, 0:W], in1=cm[:, r0:r1, :], op=ALU.add)
-
-            def emit_2():
-                nc.vector.tensor_reduce(out=st_of(0), in_=t1_of(), axis=AX.X, op=ALU.max)
-
-            def emit_3():
-                eng.tensor_tensor(
-                    out=t1_of(), in0=t1_of(), in1=st_of(0).unsqueeze(2).to_broadcast([P, n, W]), op=ALU.subtract
-                )
-
-            def emit_4():
-                nc.scalar.activation(out=ex_of(), in_=t1_of(), func=ACT.Exp)
-
-            def emit_5():
-                nc.vector.tensor_reduce(out=st_of(1), in_=ex_of(), axis=AX.X, op=ALU.add)
-                nc.vector.reciprocal(out=st_of(1), in_=st_of(1))
-
-            def emit_6():
-                eng.tensor_tensor(
-                    out=out_sb[helper][:, r0:r1, :],
-                    in0=ex_of(),
-                    in1=st_of(1).unsqueeze(2).to_broadcast([P, n, W]),
-                    op=ALU.mult,
-                )
-
-            t = add(helper, cost, deps, emit_1, -500.0, take=("soft", cs))
-            t = add("V", 0.15, [t], emit_2, -500.0)
-            t = add(helper, cost, [t], emit_3, -500.0)
-            t = add("S", 0.2, [t], emit_4, -5000.0)
-            t = add("V", 0.3, [t], emit_5, -500.0)
-            t = add(helper, cost, [t], emit_6, -500.0, give=(("soft", cs),))
-            add("D", 0.2, [t], load(out_v[:, r0:r1, :], out_sb[helper][:, r0:r1, :]), 0.0)
-
-        for r0, r1 in V_CHUNKS + G_CHUNKS:
-            softmax(r0, r1, "V" if r1 == NV else "G")
-
-        def emit_bias_t(cb):
-            def emit():
-                nc.tensor.transpose(tiles["ps"][cb["ps"]][:].bitcast(BF16)[:, 0:P], b_rows[:], ident_bf[:])
-
-            return emit
-
-        cb = {}
-        t_bt = add("T", 0.1, [t_b, t_masks], emit_bias_t(cb), -8000.0, take=("ps", cb))
-        t_bn = add(
-            "S",
-            0.1,
-            [t_bt],
-            lambda: nc.scalar.mul(out=b_nat[:], in_=tiles["ps"][cb["ps"]][:].bitcast(BF16)[:, 0:4], mul=SCALE),
-            -8000.0,
-            give=(("ps", cb),),
-        )
-
-        t_ext = []
-        prev_k = []
-        prev_q = []
-        for pi in range(NPAIR):
-            a = 8.0 + PACE_P * pi
-            cp = {}
-            b0 = T_BATCHES[2 * pi]
-            e = R // 4 + pi
-
-            def emit_lk(cp=cp, b0=b0):
-                nc.sync.dma_start(
-                    out=tiles["kb"][cp["kb"]][:], in_=k_proj[b0 : b0 + 2].rearrange("b (h p) d -> p (b h) d", p=P)
-                )
-
-            t_lk = add("N", 2.0, [add("D", 1.0, [], emit_lk, a - 4.0, take=("kb", cp))], None, 0.0)
-
-            t_kc = []
-            t_kts = []
-            cks = []
-            for be in range(2):
-                ck = {}
-                cks.append(ck)
-
-                def emit_kt2(be=be, ck=ck, cp=cp):
-                    ktb = tiles["ps"][ck["ps"]][:].bitcast(BF16).rearrange("p (c t) -> p c t", c=4)
-                    for h in range(2):
-                        for c in range(4):
-                            nc.tensor.transpose(
-                                ktb[:, c, h * P : (h + 1) * P],
-                                tiles["kb"][cp["kb"]][:, 2 * be + h, c * P : (c + 1) * P],
-                                ident_bf[:],
-                            )
-
-                def emit_kc2(ck=ck):
-                    ktb = tiles["ps"][ck["ps"]][:].bitcast(BF16).rearrange("p (c t) -> p c t", c=4)
-                    nc.scalar.copy(out=tiles["kT"][ck["kT"]][:, :, NB : NB + S], in_=ktb)
-
-                t_s = add("N", 0.0, [t_lk, t_masks, t_zero] + prev_k, None, a + 2.0 + 2.0 * be, take=("kT", ck))
-                prev_k = [t_s]
-                t_kts.append(add("T", 0.5, [t_s], emit_kt2, a + 2.0 + 2.0 * be, take=("ps", ck)))
-                t_kc.append(add("S", 0.9, [t_kts[be]], emit_kc2, a + 2.0 + 2.0 * be, give=(("ps", ck),)))
-            add("N", 0.0, t_kts, None, 0.0, give=(("kb", cp),))
-
-            t_s = add("N", 0.0, [t_qp[pi], t_wq] + prev_q, None, a + 5.0, take=("qT", cp))
-            prev_q = [t_s]
-            t_mts = []
-            t_qe = []
-            for c in range(4):
-                cc = {}
-
-                def emit_mt(c=c, cc=cc, e=e):
-                    nc.tensor.matmul_mx(
-                        out=tiles["ps"][cc["ps"]][:],
-                        lhsT=w_codes[:, c * P : (c + 1) * P].bitcast(FP8X4),
-                        lhsT_scale=w_scales[:, c * P : (c + 1) * P],
-                        rhs=codes_all[:, e, :].bitcast(FP8X4),
-                        rhs_scale=planes_all[:, e, :],
-                        start=True,
-                        stop=True,
-                    )
-
-                def emit_qe(c=c, cc=cc, cp=cp):
-                    nc.scalar.activation(
-                        out=tiles["qT"][cp["qT"]][:, c, :],
-                        in_=tiles["ps"][cc["ps"]][:],
-                        func=ACT.Identity,
-                        bias=b_nat[:, c : c + 1],
-                        scale=SCALE,
-                    )
-
-                t_mts.append(add("T", 0.23, [t_s], emit_mt, a + 5.0 + 0.5 * c, take=("ps", cc)))
-                t_qe.append(add("S", 0.5, [t_mts[c], t_bn], emit_qe, a + 5.0 + 0.5 * c, give=(("ps", cc),)))
-
-            t_bands = []
-            for be in range(2):
-                ce = {}
-                ck = cks[be]
-                tau = 4 * pi + 2 * be
-
-                def emit_bd(be=be, ce=ce, ck=ck, cp=cp):
-                    for h in range(2):
-                        for c in range(4):
-                            nc.tensor.matmul(
-                                out=tiles["sps"][ce["sps"]][:, h * BW : (h + 1) * BW],
-                                lhsT=tiles["qT"][cp["qT"]][:, c, (2 * be + h) * P : (2 * be + h + 1) * P],
-                                rhs=tiles["kT"][ck["kT"]][:, c, h * P : h * P + BW],
-                                start=(c == 0),
-                                stop=(c == 3),
-                            )
-
-                def emit_e1(ce=ce):
-                    nc.vector.tensor_tensor(
-                        out=tiles["mk"][ce["mk"]][:, :, 0:BW],
-                        in0=tiles["sps"][ce["sps"]][:, 0 : 2 * BW].rearrange("p (t n) -> p t n", t=2),
-                        in1=band01[:].unsqueeze(1).to_broadcast([P, 2, BW]),
-                        op=ALU.mult,
-                    )
-
-                def emit_e2(ce=ce, tau=tau):
-                    nc.vector.tensor_reduce(
-                        out=er2[:, tau : tau + 2, 0:W],
-                        in_=tiles["mk"][ce["mk"]][:].rearrange("p t (a m) -> p t m a", m=W),
-                        axis=AX.X,
-                        op=ALU.add,
-                    )
-
-                due = a + 8.0 + 2.0 * be
-                t_bd = add("T", 1.9, t_qe + [t_kc[be]], emit_bd, due, take=("sps", ce), give=(("kT", ck),))
-                t_bands.append(t_bd)
-                t_m = add("N", 0.0, [t_bd, t_band, t_zero], None, due, take=("mk", ce))
-                t_e1 = add("V", 0.3, [t_m], emit_e1, due, give=(("sps", ce),))
-                t_ext.append(add("V", 0.3, [t_e1], emit_e2, due + 1.0, give=(("mk", ce),)))
-            add("N", 0.0, t_bands, None, 0.0, give=(("qT", cp),))
-
-        def emit_f1():
-            nc.vector.tensor_copy(out=er2[:, :, W : 2 * W], in_=er2[:, :, 0:W])
-            nc.vector.tensor_scalar_mul(out=e_t[:], in0=er2[:, :, 0:W], scalar1=sel[:, 0:1])
-            for m in range(1, W):
+                unread = scrap.tile([P, D], F32, name="unread_v")
                 nc.vector.scalar_tensor_tensor(
-                    out=e_t[:], in0=er2[:, :, m : m + W], scalar=sel[:, m : m + 1], in1=e_t[:], op0=ALU.mult, op1=ALU.add
+                    out=unread[:],
+                    in0=q_ps[r][:],
+                    scalar=SCALE,
+                    in1=k_sb[:, r + j, :],
+                    op0=ALU.mult,
+                    op1=ALU.mult,
+                    accum_out=score[:, r, j : j + 1],
                 )
-            e_v = e_t[:].rearrange("p (b h) j -> p b (h j)", h=2)
-            nc.vector.tensor_tensor(
-                out=e_v,
-                in0=e_v,
-                in1=mask_t[:].rearrange("p h j -> p (h j)").unsqueeze(1).to_broadcast([P, NTT // 2, 2 * W]),
-                op=ALU.add,
+
+        def gpsimd_tile(m):
+            r = R - 1 - m
+            bank = ps_short.tile([P, D], F32, name="bank")
+            q_tokens(r, bank)
+            q_sb = two.tile([P, D], F32, name="q_sb")
+            nc.scalar.mul(out=q_sb[:], in_=bank[:], mul=SCALE)
+            prod[m] = two.tile([P, W, D], F32, name="prod")
+            for j in range(W):
+                nc.gpsimd.tensor_tensor(out=prod[m][:, j, :], in0=q_sb[:], in1=k_sb[:, r + j, :], op=ALU.mult)
+
+        def gpsimd_sums(m, j0, j1):
+            for j in range(j0, j1):
+                unread = scrap.tile([P, D], BF16, name="unread_s")
+                nc.scalar.activation(
+                    out=unread[:], in_=prod[m][:, j, :], func=ACT.Copy, accum_out=score[:, R - 1 - m, j : j + 1]
+                )
+
+        def c_transpose(i):
+            bank = ps_short.tile([P, 512], F32, name="bank")
+            halves = bank[:].rearrange("p (i u t) -> p i u t", i=2, u=2)
+            for n in range(2):
+                for u in range(2):
+                    nc.tensor.transpose(halves[:, n, u, :], k_words[:, 2 * i + n, u * P : (u + 1) * P], ident[:])
+            kt_sb[i] = two.tile([P, 512], F32, name="kt_sb")
+            nc.scalar.copy(out=kt_sb[i][:], in_=bank[:])
+
+        def c_dot(i):
+            values = kt_sb[i][:].bitcast(BF16).rearrange("p (i u t e) -> p i u t e", i=2, u=2, e=2)
+            for n in range(2):
+                for v in range(4):
+                    nc.tensor.matmul(
+                        out=c_ps[:, 2 * i + n : 2 * i + n + 1],
+                        lhsT=values[:, n, v // 2, :, v % 2],
+                        rhs=b_words[:, v : v + 1],
+                        start=(v == 0),
+                        stop=(v == 3),
+                    )
+
+        def band_keys(pi, be):
+            bank = ps_short.tile([P, 512], F32, name="bank")
+            chunks = bank[:].bitcast(BF16).rearrange("p (c t) -> p c t", c=4)
+            for h in range(2):
+                for c in range(4):
+                    nc.tensor.transpose(
+                        chunks[:, c, h * P : (h + 1) * P], kb_in[pi][:, 2 * be + h, c * P : (c + 1) * P], ident_bf[:]
+                    )
+            nc.scalar.copy(out=keys_t[(2 * pi + be) % 3][:, :, NB : NB + S], in_=chunks)
+
+        def band_q(pi, c):
+            if c == 0:
+                q_t[pi] = two.tile([P, 4, 4 * P], F32, name="q_t")
+            bank = ps_short.tile([P, 512], F32, name="bank")
+            nc.tensor.matmul_mx(
+                out=bank[:],
+                lhsT=w_codes[:, c * P : (c + 1) * P].bitcast(FP8X4),
+                lhsT_scale=w_scales[:, c * P : (c + 1) * P],
+                rhs=x_codes[:, R // 4 + pi, :].bitcast(FP8X4),
+                rhs_scale=x_scales[:, R // 4 + pi, :],
+                start=True,
+                stop=True,
             )
-            nc.vector.tensor_reduce(out=st_t[:, 0, :], in_=e_t[:], axis=AX.X, op=ALU.max)
-            nc.vector.tensor_tensor(
-                out=e_t[:], in0=e_t[:], in1=st_t[:, 0, :].unsqueeze(2).to_broadcast([P, NTT, W]), op=ALU.subtract
+            nc.scalar.activation(
+                out=q_t[pi][:, c, :], in_=bank[:], func=ACT.Identity, bias=b_part[:, c : c + 1], scale=SCALE
             )
 
-        def emit_f3():
-            nc.vector.tensor_reduce(out=st_t[:, 1, :], in_=x_t[:], axis=AX.X, op=ALU.add)
-            nc.vector.reciprocal(out=st_t[:, 1, :], in_=st_t[:, 1, :])
+        def band_scores(pi, be):
+            for h in range(2):
+                for c in range(4):
+                    nc.tensor.matmul(
+                        out=band_ps[:, h * BW : (h + 1) * BW],
+                        lhsT=q_t[pi][:, c, (2 * be + h) * P : (2 * be + h + 1) * P],
+                        rhs=keys_t[(2 * pi + be) % 3][:, c, h * P : h * P + BW],
+                        start=(c == 0),
+                        stop=(c == 3),
+                    )
+
+        def band_pick(pi, be):
+            keep = kept[be]
             nc.vector.tensor_tensor(
-                out=p_t[:, :, 0 : W * NTT // 2].rearrange("p g (t j) -> p g t j", j=W),
-                in0=x_t[:].rearrange("p (g t) j -> p g t j", g=2),
-                in1=st_t[:, 1, :].rearrange("p (g t) -> p g t", g=2).unsqueeze(3).to_broadcast([P, 2, NTT // 2, W]),
+                out=keep[:, :, 0:BW],
+                in0=band_ps.rearrange("p (t n) -> p t n", t=2),
+                in1=band01[:].unsqueeze(1).to_broadcast([P, 2, BW]),
                 op=ALU.mult,
             )
-
-        cf = {}
-        cg = {}
-
-        def emit_f4():
-            for g in range(2):
-                nc.tensor.transpose(tiles["ps"][cf["ps"]][:, g * P : (g + 1) * P], p_t[:, g, :], ident[:])
-
-        def emit_f6():
-            for e in range(2):
-                nc.tensor.transpose(tiles["ps"][cg["ps"]][:, e * P : (e + 1) * P], t1_sb[:, e : 2 * P : 2], ident[:])
-
-        def emit_f7():
-            nc.scalar.copy(
-                out=f_sb[:],
-                in_=tiles["ps"][cg["ps"]][:, 0 : 2 * P]
-                .rearrange("p (e c) -> p e c", e=2)[:, :, 0 : W * NTT // 2]
-                .rearrange("p e (t j) -> p t e j", j=W),
+            tau = 4 * pi + 2 * be
+            nc.vector.tensor_reduce(
+                out=picked[:, tau : tau + 2, 0:W],
+                in_=keep[:].rearrange("p t (a m) -> p t m a", m=W),
+                axis=AX.X,
+                op=ALU.add,
             )
 
-        def emit_f8():
+        def soft_shift(r0, r1):
+            n = r1 - r0
+            s = two.tile([P, 12, W], F32, name="soft_s")
+            m = two.tile([P, 2, 12], F32, name="soft_m")
+            soft[r0] = (s, two.tile([P, 12, W], F32, name="soft_e"), m)
+            nc.vector.tensor_tensor(out=s[:, 0:n, :], in0=score[:, r0:r1, 0:W], in1=c_mask[:, r0:r1, :], op=ALU.add)
+            nc.vector.tensor_reduce(out=m[:, 0, 0:n], in_=s[:, 0:n, :], axis=AX.X, op=ALU.max)
+            nc.vector.tensor_tensor(
+                out=s[:, 0:n, :], in0=s[:, 0:n, :], in1=m[:, 0, 0:n].unsqueeze(2).to_broadcast([P, n, W]), op=ALU.subtract
+            )
+
+        def soft_exp(r0, r1):
+            n = r1 - r0
+            s, e, m = soft[r0]
+            nc.scalar.activation(out=e[:, 0:n, :], in_=s[:, 0:n, :], func=ACT.Exp)
+
+        def soft_norm(r0, r1):
+            n = r1 - r0
+            s, e, m = soft[r0]
+            nc.vector.tensor_reduce(out=m[:, 1, 0:n], in_=e[:, 0:n, :], axis=AX.X, op=ALU.add)
+            nc.vector.reciprocal(out=m[:, 1, 0:n], in_=m[:, 1, 0:n])
+            nc.vector.tensor_tensor(
+                out=out_sb[:, r0:r1, :], in0=e[:, 0:n, :], in1=m[:, 1, 0:n].unsqueeze(2).to_broadcast([P, n, W]), op=ALU.mult
+            )
+            nc.sync.dma_start(out=out_rows[:, r0:r1, :], in_=out_sb[:, r0:r1, :])
+
+        def band_soft_exp():
+            nc.vector.tensor_copy(out=picked[:, :, W : 2 * W], in_=picked[:, :, 0:W])
+            nc.vector.tensor_scalar_mul(out=band_s[:], in0=picked[:, :, 0:W], scalar1=turned[:, 0:1])
+            for m in range(1, W):
+                nc.vector.scalar_tensor_tensor(
+                    out=band_s[:],
+                    in0=picked[:, :, m : m + W],
+                    scalar=turned[:, m : m + 1],
+                    in1=band_s[:],
+                    op0=ALU.mult,
+                    op1=ALU.add,
+                )
+            by_batch = band_s[:].rearrange("p (b h) j -> p b (h j)", h=2)
+            nc.vector.tensor_tensor(
+                out=by_batch,
+                in0=by_batch,
+                in1=edge[:].rearrange("p h j -> p (h j)").unsqueeze(1).to_broadcast([P, BAND_TILES // 2, 2 * W]),
+                op=ALU.add,
+            )
+            nc.vector.tensor_reduce(out=band_m[:, 0, :], in_=band_s[:], axis=AX.X, op=ALU.max)
+            nc.vector.tensor_tensor(
+                out=band_s[:],
+                in0=band_s[:],
+                in1=band_m[:, 0, :].unsqueeze(2).to_broadcast([P, BAND_TILES, W]),
+                op=ALU.subtract,
+            )
+            nc.scalar.activation(out=band_e[:], in_=band_s[:], func=ACT.Exp)
+
+        def band_soft_norm():
+            half = BAND_TILES // 2
+            nc.vector.tensor_reduce(out=band_m[:, 1, :], in_=band_e[:], axis=AX.X, op=ALU.add)
+            nc.vector.reciprocal(out=band_m[:, 1, :], in_=band_m[:, 1, :])
+            nc.vector.tensor_tensor(
+                out=band_p[:, :, 0 : W * half].rearrange("p g (t j) -> p g t j", j=W),
+                in0=band_e[:].rearrange("p (g t) j -> p g t j", g=2),
+                in1=band_m[:, 1, :].rearrange("p (g t) -> p g t", g=2).unsqueeze(3).to_broadcast([P, 2, half, W]),
+                op=ALU.mult,
+            )
+            bank = ps_short.tile([P, 512], F32, name="bank")
             for g in range(2):
-                t0 = T_RANGES[g][0] * S
+                nc.tensor.transpose(bank[:, g * P : (g + 1) * P], band_p[:, g, :], ident[:])
+            nc.scalar.copy(out=band_t[:], in_=bank[:, 0 : 2 * P])
+
+        def band_store():
+            half = BAND_TILES // 2
+            bank = ps_short.tile([P, 512], F32, name="bank")
+            for e in range(2):
+                nc.tensor.transpose(bank[:, e * P : (e + 1) * P], band_t[:, e : 2 * P : 2], ident[:])
+            nc.scalar.copy(
+                out=band_o[:],
+                in_=bank[:, 0 : 2 * P]
+                .rearrange("p (e c) -> p e c", e=2)[:, :, 0 : W * half]
+                .rearrange("p e (t j) -> p t e j", j=W),
+            )
+            for g in range(2):
+                t0 = BAND_FIRST[g] * S
                 nc.sync.dma_start(
-                    out=out_f[t0 : t0 + NTT // 2 * P, :].rearrange("(t u e) j -> u t (e j)", t=NTT // 2, e=2),
-                    in_=f_sb[g * 64 : (g + 1) * 64].rearrange("u t e j -> u t (e j)"),
+                    out=out_f[t0 : t0 + half * P, :].rearrange("(t u e) j -> u t (e j)", t=half, e=2),
+                    in_=band_o[g * 64 : (g + 1) * 64].rearrange("u t e j -> u t (e j)"),
                 )
 
-        t_f1 = add("V", 1.8, t_ext + [t_masks], emit_f1, -400.0)
-        t_f2 = add("S", 0.25, [t_f1], lambda: nc.scalar.activation(out=x_t[:], in_=e_t[:], func=ACT.Exp), -5000.0)
-        t_f3 = add("V", 0.6, [t_f2, t_zero], emit_f3, -400.0)
-        t_f4 = add("T", 0.2, [t_f3], emit_f4, -400.0, take=("ps", cf))
-        t_f5 = add(
-            "S",
-            0.3,
-            [t_f4],
-            lambda: nc.scalar.copy(out=t1_sb[:], in_=tiles["ps"][cf["ps"]][:, 0 : 2 * P]),
-            -5000.0,
-            give=(("ps", cf),),
-        )
-        t_f6 = add("T", 0.25, [t_f5], emit_f6, -400.0, take=("ps", cg))
-        t_f7 = add("S", 0.25, [t_f6], emit_f7, -5000.0, give=(("ps", cg),))
-        add("D", 0.4, [t_f7], emit_f8, 0.0)
+        def burst(b):
+            groups = [b] if b <= (NV - 1) // 4 else []
+            if b < PAIRS:
+                groups.append(R // 4 + b)
+            if b % 2 == 1 and b // 2 < NG // 4:
+                groups.append(R // 4 - 1 - b // 2)
+            return groups
 
-        run_schedule(tasks, slots)
+        nc.sync.dma_start(out=w_sb[:], in_=Wq.rearrange("(c p) d -> p c d", p=P))
+        load_x(0)
+        load_x(R // 4)
+        for g in (0, 1):
+            load_keys(g)
+        load_band_keys(0)
+        for e in burst(1):
+            load_x(e)
+        for g in (10, 9):
+            load_keys(g)
+        load_band_keys(1)
+
+        make_identity(nc, ident[:])
+        nc.gpsimd.iota(place[:], pattern=[[1, R]], base=0, channel_multiplier=R)
+        nc.gpsimd.memset(band01[:], 0.0)
+        for j in range(W):
+            nc.gpsimd.tensor_tensor(out=band01[:, j : j + P], in0=band01[:, j : j + P], in1=ident[:], op=ALU.add)
+
+        nc.vector.memset(b_rows[:], 0.0)
+        with nc.allow_non_contiguous_dma(reason="bias, two neighbouring values to a partition"):
+            nc.scalar.dma_start(
+                out=b_words[:].rearrange("w (u e) -> w u e", e=2), in_=bq.rearrange("(u w e) -> w u e", u=2, e=2)
+            )
+        nc.scalar.dma_start(out=b_rows[0:4, :], in_=bq.rearrange("(c p) -> c p", p=P))
+        nc.vector.memset(mask[:], 0.0)
+        nc.vector.memset(edge[:], 0.0)
+        nc.vector.memset(band_p[:], 0.0)
+        for t in keys_t:
+            nc.vector.memset(t[:, :, 0:NB], 0.0)
+            nc.vector.memset(t[:, :, NB + S : 2 * NB + S], 0.0)
+        for t in kept:
+            nc.vector.memset(t[:, :, BW : BW + 3], 0.0)
+        nc.vector.tensor_copy(out=ident_bf[:], in_=ident[:])
+        for i in range(W):
+            nc.vector.tensor_reduce(out=turned[:, i : i + 1], in_=ident[:, i:P:W], axis=AX.X, op=ALU.add)
+        nc.vector.tensor_reduce(out=edge[:, 0, 0:1], in_=ident[:, 0:2], axis=AX.X, op=ALU.add)
+        nc.vector.tensor_copy(out=edge[:, 0, 1:2], in_=ident[:, 0:1])
+        nc.vector.tensor_copy(out=edge[:, 1, 3:4], in_=ident[:, P - 1 : P])
+        nc.vector.tensor_reduce(out=edge[:, 1, 4:5], in_=ident[:, P - 2 : P], axis=AX.X, op=ALU.add)
+        nc.vector.tensor_scalar_mul(out=edge[:], in0=edge[:], scalar1=NEG)
+        nc.vector.tensor_single_scalar(out=place[:], in_=place[:], scalar=S - 1, op=ALU.bitwise_and)
+        nc.vector.tensor_copy(out=place_f[:], in_=place[:])
+        for j, op, bound in ((0, ALU.is_lt, 2.0), (1, ALU.is_lt, 1.0), (3, ALU.is_gt, S - 2.0), (4, ALU.is_gt, S - 3.0)):
+            nc.vector.tensor_scalar(out=mask[:, :, j], in0=place_f[:], scalar1=bound, scalar2=NEG, op0=op, op1=ALU.mult)
+
+        quantise(pack_four(lambda i: w_sb[:].bitcast(F32)[:, i, :], nc.vector.tensor_copy), w_codes[:], w_scales[:])
+        stage_x(0)
+        stage_x(R // 4)
+        quantise_x(0)
+        vector_q(0)
+        vector_q(1)
+        quantise_x(R // 4)
+        bank = ps_short.tile([P, 512], F32, name="bank")
+        nc.tensor.transpose(bank[:].bitcast(BF16)[:, 0:P], b_rows[:], ident_bf[:])
+        nc.scalar.mul(out=b_part[:], in_=bank[:].bitcast(BF16)[:, 0:4], mul=SCALE)
+
+        for t in range(-2, LAST_STEP + 1):
+            b = turn(t, -10, 4, 7)
+            if b is not None and b >= 2:
+                for e in burst(b):
+                    load_x(e)
+            pi = turn(t, -8, 4, PAIRS)
+            if pi is not None and pi >= 2:
+                load_band_keys(pi)
+            n = turn(t, -1, 1, len(LATER_KEYS))
+            if n is not None:
+                load_keys(LATER_KEYS[n])
+
+            if t == HR // 2 + 1:
+                nc.scalar.mul(out=c_sb[:], in_=c_ps, mul=SCALE)
+                for j in range(W):
+                    nc.gpsimd.tensor_tensor(out=c_mask[:, :, j], in0=c_sb[:, j : j + R], in1=mask[:, :, j], op=ALU.add)
+            if t == 4 * PAIRS + 2:
+                band_soft_exp()
+            if t == 4 * PAIRS + 3:
+                band_soft_norm()
+            if t == 4 * PAIRS + 4:
+                band_store()
+            for first, r0, r1 in SOFT_CHUNKS:
+                for n, stage_of_softmax in enumerate((soft_shift, soft_exp, soft_norm)):
+                    if t == first + n:
+                        stage_of_softmax(r0, r1)
+
+            for be in range(2):
+                pi = turn(t, 2 * be + 2, 4, PAIRS)
+                if pi is not None:
+                    band_scores(pi, be)
+                pi = turn(t, 2 * be + 3, 4, PAIRS)
+                if pi is not None:
+                    band_pick(pi, be)
+
+            b = turn(t, -2, 4, 7)
+            if b is not None and b >= 1:
+                for e in burst(b):
+                    quantise_x(e)
+            for n in range(3):
+                b = turn(t, n - 6, 4, 7)
+                if b is not None and b >= 1 and n < len(burst(b)):
+                    stage_x(burst(b)[n])
+
+            m = turn(t, 3, 2, NG)
+            if m is not None:
+                gpsimd_tile(m)
+
+            i = turn(t, 1, 1, HR // 2)
+            if i is not None:
+                c_dot(i)
+            i = turn(t, 0, 1, HR // 2)
+            if i is not None:
+                c_transpose(i)
+
+            for be in range(2):
+                pi = turn(t, be - 2, 4, PAIRS)
+                if pi is not None:
+                    band_keys(pi, be)
+                pi = turn(t, be, 4, PAIRS)
+                if pi is not None:
+                    band_q(pi, 2 * be)
+                    band_q(pi, 2 * be + 1)
+
+            if 2 <= t + 2 < NV:
+                vector_q(t + 2)
+
+            m = turn(t, 5, 2, NG)
+            if m is not None:
+                gpsimd_sums(m, 0, 3)
+            m = turn(t, 6, 2, NG)
+            if m is not None:
+                gpsimd_sums(m, 3, W)
+
+            if 0 <= t < NV:
+                vector_tile(t)

@@ -61,7 +61,7 @@ def tile_crosssliceattention_pa_t_kernel(tc, x, Wq, bq, k_proj, out):
         stage = ctx.enter_context(tc.tile_pool(name="stage", bufs=3))
         two = ctx.enter_context(tc.tile_pool(name="two", bufs=2))
         scrap = ctx.enter_context(tc.tile_pool(name="scrap", bufs=4))
-        ps_short = ctx.enter_context(tc.psum_pool(name="ps_short", bufs=3))
+        ps_short = ctx.enter_context(tc.psum_pool(name="ps_short", bufs=4))
         ps_q = ctx.enter_context(tc.psum_pool(name="ps_q", bufs=3))
         ps_fixed = ctx.enter_context(tc.psum_pool(name="ps_fixed", bufs=1))
         ctx.enter_context(tc.manual_schedule())
@@ -96,8 +96,9 @@ def tile_crosssliceattention_pa_t_kernel(tc, x, Wq, bq, k_proj, out):
         band_o = fixed.tile([P, BAND_TILES // 2, 2, W], F32, name="band_o")
         keys_t = [fixed.tile([P, 4, S + 2 * NB], F32, name="keys_t%d" % i) for i in range(3)]
         kept = [fixed.tile([P, 2, BW + 3], F32, name="kept%d" % i) for i in range(2)]
-        band_ps = ps_fixed.tile([P, 2 * BW], F32, name="band_ps")[:]
-        c_ps = ps_fixed.tile([P, HR], F32, name="c_ps")[:]
+        shared = ps_fixed.tile([P, 512], F32, name="shared")
+        band_ps = shared[:, 0 : 2 * BW]
+        c_ps = shared[:, 2 * BW : 2 * BW + HR]
 
         k_words = k_sb[:].bitcast(F32)
         x_in, grouped, q_ps, prod, kb_in, kt_sb, q_t, soft = {}, {}, {}, {}, {}, {}, {}, {}
@@ -185,8 +186,8 @@ def tile_crosssliceattention_pa_t_kernel(tc, x, Wq, bq, k_proj, out):
             for j in range(W):
                 nc.gpsimd.tensor_tensor(out=prod[m][:, j, :], in0=q_sb[:], in1=k_sb[:, r + j, :], op=ALU.mult)
 
-        def gpsimd_sums(m, j0, j1):
-            for j in range(j0, j1):
+        def gpsimd_sums(m):
+            for j in range(W):
                 unread = scrap.tile([P, D], BF16, name="unread_s")
                 nc.scalar.activation(
                     out=unread[:], in_=prod[m][:, j, :], func=ACT.Copy, accum_out=score[:, R - 1 - m, j : j + 1]
@@ -445,52 +446,47 @@ def tile_crosssliceattention_pa_t_kernel(tc, x, Wq, bq, k_proj, out):
                     if t == first + n:
                         stage_of_softmax(r0, r1)
 
-            for be in range(2):
-                pi = turn(t, 2 * be + 2, 4, PAIRS)
-                if pi is not None:
-                    band_scores(pi, be)
-                pi = turn(t, 2 * be + 3, 4, PAIRS)
-                if pi is not None:
-                    band_pick(pi, be)
-
             b = turn(t, -2, 4, 7)
             if b is not None and b >= 1:
                 for e in burst(b):
                     quantise_x(e)
+
             for n in range(3):
                 b = turn(t, n - 6, 4, 7)
                 if b is not None and b >= 1 and n < len(burst(b)):
                     stage_x(burst(b)[n])
-
-            m = turn(t, 3, 2, NG)
-            if m is not None:
-                gpsimd_tile(m)
-
-            i = turn(t, 1, 1, HR // 2)
-            if i is not None:
-                c_dot(i)
             i = turn(t, 0, 1, HR // 2)
             if i is not None:
                 c_transpose(i)
-
             for be in range(2):
                 pi = turn(t, be - 2, 4, PAIRS)
                 if pi is not None:
                     band_keys(pi, be)
+            i = turn(t, 1, 1, HR // 2)
+            if i is not None:
+                c_dot(i)
+            for be in range(2):
+                pi = turn(t, 2 * be + 2, 4, PAIRS)
+                if pi is not None:
+                    band_scores(pi, be)
+            for be in range(2):
                 pi = turn(t, be, 4, PAIRS)
                 if pi is not None:
                     band_q(pi, 2 * be)
                     band_q(pi, 2 * be + 1)
-
+            m = turn(t, 3, 2, NG)
+            if m is not None:
+                gpsimd_tile(m)
             if 2 <= t + 2 < NV:
                 vector_q(t + 2)
 
             m = turn(t, 5, 2, NG)
             if m is not None:
-                gpsimd_sums(m, 0, 3)
-            m = turn(t, 6, 2, NG)
-            if m is not None:
-                gpsimd_sums(m, 3, W)
+                gpsimd_sums(m)
 
             if 0 <= t < NV:
                 vector_tile(t)
+            for be in range(2):
+                pi = turn(t, 2 * be + 3, 4, PAIRS)
+                if pi is not None:
+                    band_pick(pi, be)

import math
from contextlib import ExitStack

import concourse.mybir as mybir
from concourse.masks import make_identity

F32 = mybir.dt.float32
BF16 = mybir.dt.bfloat16
I32 = mybir.dt.int32
U32 = mybir.dt.uint32
U8 = mybir.dt.uint8
FP8X4 = mybir.dt.float8_e4m3fn_x4
ALU = mybir.AluOpType
ACT = mybir.ActivationFunctionType
AX = mybir.AxisListType

P = 128
B, S, D = 32, 256, 512
W = 5
NB = 2
SCALE = 1.0 / math.sqrt(D)
NEG = -1.0e30

BAND_FIRST = (0, 26)
BAND_BATCHES = 6
PAIRS = BAND_BATCHES
BAND_TILES = 4 * PAIRS
BW = P + 2 * NB
R = 40
HR = R + 2 * NB
TOK0 = BAND_BATCHES * S
NTOK = R * P
NV = 28
NG = R - NV
GROUPS = R // 4 + PAIRS
LAST_STEP = NV + 3
SOFT_CHUNKS = ((24, 0, 12), (24, 12, 24), (NV + 1, NV, R), (NV, 24, NV))
LATER_KEYS = (2, 3, 8, 4, 5, 7, 6)

FLOPS = 2 * B * S * D * D + 2 * B * S * W * D


def turn(t, first, period, count):
    n, rest = divmod(t - first, period)
    return n if rest == 0 and 0 <= n < count else None


def tile_crosssliceattention_pa_t_kernel(tc, x, Wq, bq, k_proj, out):
    nc = tc.nc
    x_f = x.flatten_outer_dims()
    k_f = k_proj.flatten_outer_dims()
    out_f = out.flatten_outer_dims()
    x_rows = x_f[TOK0 : TOK0 + NTOK, :].rearrange("(p r) d -> p r d", r=R)
    k_rows = k_f[TOK0 - NB : TOK0 - NB + NTOK, :].rearrange("(p r) d -> p r d", r=R)
    k_tail = k_f[TOK0 - NB + R : TOK0 - NB + R + NTOK, :].rearrange("(p r) d -> p r d", r=R)
    out_rows = out_f[TOK0 : TOK0 + NTOK, :].rearrange("(p r) j -> p r j", r=R)

    with ExitStack() as ctx:
        fixed = ctx.enter_context(tc.tile_pool(name="fixed", bufs=1))
        x_pool = ctx.enter_context(tc.tile_pool(name="x_pool", bufs=6))
        stage = ctx.enter_context(tc.tile_pool(name="stage", bufs=3))
        two = ctx.enter_context(tc.tile_pool(name="two", bufs=2))
        scrap = ctx.enter_context(tc.tile_pool(name="scrap", bufs=4))
        ps_short = ctx.enter_context(tc.psum_pool(name="ps_short", bufs=4))
        ps_q = ctx.enter_context(tc.psum_pool(name="ps_q", bufs=3))
        ps_fixed = ctx.enter_context(tc.psum_pool(name="ps_fixed", bufs=1))
        ctx.enter_context(tc.manual_schedule())

        ident = fixed.tile([P, P], F32, name="ident")
        ident_bf = fixed.tile([P, P], BF16, name="ident_bf")
        k_sb = fixed.tile([P, HR, D], BF16, name="k_sb")
        w_sb = fixed.tile([P, 4, D], BF16, name="w_sb")
        w_codes = fixed.tile([P, D], U32, align_bytes=64, name="w_codes")
        w_scales = fixed.tile([P, D], U8, align_bytes=64, name="w_scales")
        x_codes = fixed.tile([P, GROUPS, 4 * P], U32, align_bytes=64, name="x_codes")
        x_scales = fixed.tile([P, GROUPS, 4 * P], U8, align_bytes=64, name="x_scales")
        b_words = fixed.tile([P, 4], BF16, name="b_words")
        b_rows = fixed.tile([P, P], BF16, name="b_rows")
        b_part = fixed.tile([P, 4], F32, name="b_part")
        score = fixed.tile([P, R, 8], F32, name="score")
        c_sb = fixed.tile([P, HR], F32, name="c_sb")
        c_mask = fixed.tile([P, R, W], F32, name="c_mask")
        mask = fixed.tile([P, R, W], F32, name="mask")
        place = fixed.tile([P, R], I32, name="place")
        place_f = fixed.tile([P, R], F32, name="place_f")
        out_sb = fixed.tile([P, R, W], F32, name="out_sb")
        band01 = fixed.tile([P, BW], F32, name="band01")
        turned = fixed.tile([P, W], F32, name="turned")
        edge = fixed.tile([P, 2, W], F32, name="edge")
        picked = fixed.tile([P, BAND_TILES, 2 * W], F32, name="picked")
        band_s = fixed.tile([P, BAND_TILES, W], F32, name="band_s")
        band_e = fixed.tile([P, BAND_TILES, W], F32, name="band_e")
        band_m = fixed.tile([P, 2, BAND_TILES], F32, name="band_m")
        band_p = fixed.tile([P, 2, P], F32, name="band_p")
        band_t = fixed.tile([P, 2 * P], F32, name="band_t")
        band_o = fixed.tile([P, BAND_TILES // 2, 2, W], F32, name="band_o")
        keys_t = [fixed.tile([P, 4, S + 2 * NB], F32, name="keys_t%d" % i) for i in range(3)]
        kept = [fixed.tile([P, 2, BW + 3], F32, name="kept%d" % i) for i in range(2)]
        shared = ps_fixed.tile([P, 512], F32, name="shared")
        band_ps = shared[:, 0 : 2 * BW]
        c_ps = shared[:, 2 * BW : 2 * BW + HR]

        k_words = k_sb[:].bitcast(F32)
        x_in, grouped, q_ps, prod, kb_in, kt_sb, q_t, soft = {}, {}, {}, {}, {}, {}, {}, {}

        def load_keys(g):
            src = k_rows[:, 4 * g : 4 * g + 4, :] if g < R // 4 else k_tail[:, 0:4, :]
            nc.sync.dma_start(out=k_sb[:, 4 * g : 4 * g + 4, :], in_=src)

        def pair_batch(pi):
            return BAND_FIRST[pi // 3] + 2 * (pi % 3)

        def load_x(e):
            x_in[e] = x_pool.tile([P, 4, D], BF16, name="x_in")
            if e < R // 4:
                src = x_rows[:, 4 * e : 4 * e + 4, :]
            else:
                b0 = pair_batch(e - R // 4)
                src = x[b0 : b0 + 2].rearrange("b (h p) d -> p (b h) d", p=P)
            nc.sync.dma_start(out=x_in[e][:], in_=src)

        def load_band_keys(pi):
            b0 = pair_batch(pi)
            kb_in[pi] = two.tile([P, 4, D], BF16, name="kb_in")
            nc.sync.dma_start(out=kb_in[pi][:], in_=k_proj[b0 : b0 + 2].rearrange("b (h p) d -> p (b h) d", p=P))

        def pack_four(words_of, copy):
            packed = stage.tile([P, 4 * P, 4], BF16, align_bytes=64, name="packed")
            packed_words = packed[:].bitcast(F32)
            for h in range(2):
                bank = ps_short.tile([P, 512], F32, name="bank")
                halves = bank[:].rearrange("p (i u t) -> p i u t", i=2, u=2)
                for i in range(2):
                    for u in range(2):
                        nc.tensor.transpose(halves[:, i, u, :], words_of(2 * h + i)[:, u * P : (u + 1) * P], ident[:])
                copy(
                    out=packed_words[:, 2 * h * P : (2 * h + 2) * P, :].rearrange("p (i t) u -> p i t u", i=2),
                    in_=halves.rearrange("p i u t -> p i t u"),
                )
            return packed

        def quantise(packed, codes, scales):
            nc.vector.quantize_mx(out=codes.bitcast(FP8X4), scales=scales, in_=packed[:].rearrange("p t j -> p (t j)"))

        def stage_x(e):
            grouped[e] = pack_four(lambda i: x_in[e][:].bitcast(F32)[:, i, :], nc.scalar.copy)

        def quantise_x(e):
            quantise(grouped[e], x_codes[:, e, :], x_scales[:, e, :])

        def q_tokens(r, bank):
            nc.tensor.matmul_mx(
                out=bank[:],
                lhsT=x_codes[:, r // 4, (r % 4) * P : (r % 4 + 1) * P].bitcast(FP8X4),
                lhsT_scale=x_scales[:, r // 4, (r % 4) * P : (r % 4 + 1) * P],
                rhs=w_codes[:].bitcast(FP8X4),
                rhs_scale=w_scales[:],
                start=True,
                stop=True,
            )

        def vector_q(r):
            q_ps[r] = ps_q.tile([P, D], F32, name="q_ps")
            q_tokens(r, q_ps[r])

        def vector_tile(r):
            for j in range(W):
                unread = scrap.tile([P, D], F32, name="unread_v")
                nc.vector.scalar_tensor_tensor(
                    out=unread[:],
                    in0=q_ps[r][:],
                    scalar=SCALE,
                    in1=k_sb[:, r + j, :],
                    op0=ALU.mult,
                    op1=ALU.mult,
                    accum_out=score[:, r, j : j + 1],
                )

        def gpsimd_tile(m):
            r = R - 1 - m
            bank = ps_short.tile([P, D], F32, name="bank")
            q_tokens(r, bank)
            q_sb = two.tile([P, D], F32, name="q_sb")
            nc.scalar.mul(out=q_sb[:], in_=bank[:], mul=SCALE)
            prod[m] = two.tile([P, W, D], F32, name="prod")
            for j in range(W):
                nc.gpsimd.tensor_tensor(out=prod[m][:, j, :], in0=q_sb[:], in1=k_sb[:, r + j, :], op=ALU.mult)

        def gpsimd_sums(m):
            for j in range(W):
                unread = scrap.tile([P, D], BF16, name="unread_s")
                nc.scalar.activation(
                    out=unread[:], in_=prod[m][:, j, :], func=ACT.Copy, accum_out=score[:, R - 1 - m, j : j + 1]
                )

        def c_transpose(i):
            bank = ps_short.tile([P, 512], F32, name="bank")
            halves = bank[:].rearrange("p (i u t) -> p i u t", i=2, u=2)
            for n in range(2):
                for u in range(2):
                    nc.tensor.transpose(halves[:, n, u, :], k_words[:, 2 * i + n, u * P : (u + 1) * P], ident[:])
            kt_sb[i] = two.tile([P, 512], F32, name="kt_sb")
            nc.scalar.copy(out=kt_sb[i][:], in_=bank[:])

        def c_dot(i):
            values = kt_sb[i][:].bitcast(BF16).rearrange("p (i u t e) -> p i u t e", i=2, u=2, e=2)
            for n in range(2):
                for v in range(4):
                    nc.tensor.matmul(
                        out=c_ps[:, 2 * i + n : 2 * i + n + 1],
                        lhsT=values[:, n, v // 2, :, v % 2],
                        rhs=b_words[:, v : v + 1],
                        start=(v == 0),
                        stop=(v == 3),
                    )

        def band_keys(pi, be):
            bank = ps_short.tile([P, 512], F32, name="bank")
            chunks = bank[:].bitcast(BF16).rearrange("p (c t) -> p c t", c=4)
            for h in range(2):
                for c in range(4):
                    nc.tensor.transpose(
                        chunks[:, c, h * P : (h + 1) * P], kb_in[pi][:, 2 * be + h, c * P : (c + 1) * P], ident_bf[:]
                    )
            nc.scalar.copy(out=keys_t[(2 * pi + be) % 3][:, :, NB : NB + S], in_=chunks)

        def band_q(pi, c):
            if c == 0:
                q_t[pi] = two.tile([P, 4, 4 * P], F32, name="q_t")
            bank = ps_short.tile([P, 512], F32, name="bank")
            nc.tensor.matmul_mx(
                out=bank[:],
                lhsT=w_codes[:, c * P : (c + 1) * P].bitcast(FP8X4),
                lhsT_scale=w_scales[:, c * P : (c + 1) * P],
                rhs=x_codes[:, R // 4 + pi, :].bitcast(FP8X4),
                rhs_scale=x_scales[:, R // 4 + pi, :],
                start=True,
                stop=True,
            )
            nc.scalar.activation(
                out=q_t[pi][:, c, :], in_=bank[:], func=ACT.Identity, bias=b_part[:, c : c + 1], scale=SCALE
            )

        def band_scores(pi, be):
            for h in range(2):
                for c in range(4):
                    nc.tensor.matmul(
                        out=band_ps[:, h * BW : (h + 1) * BW],
                        lhsT=q_t[pi][:, c, (2 * be + h) * P : (2 * be + h + 1) * P],
                        rhs=keys_t[(2 * pi + be) % 3][:, c, h * P : h * P + BW],
                        start=(c == 0),
                        stop=(c == 3),
                    )

        def band_pick(pi, be):
            keep = kept[be]
            nc.vector.tensor_tensor(
                out=keep[:, :, 0:BW],
                in0=band_ps.rearrange("p (t n) -> p t n", t=2),
                in1=band01[:].unsqueeze(1).to_broadcast([P, 2, BW]),
                op=ALU.mult,
            )
            tau = 4 * pi + 2 * be
            nc.vector.tensor_reduce(
                out=picked[:, tau : tau + 2, 0:W],
                in_=keep[:].rearrange("p t (a m) -> p t m a", m=W),
                axis=AX.X,
                op=ALU.add,
            )

        def soft_shift(r0, r1):
            n = r1 - r0
            s = two.tile([P, 12, W], F32, name="soft_s")
            m = two.tile([P, 2, 12], F32, name="soft_m")
            soft[r0] = (s, two.tile([P, 12, W], F32, name="soft_e"), m)
            nc.vector.tensor_tensor(out=s[:, 0:n, :], in0=score[:, r0:r1, 0:W], in1=c_mask[:, r0:r1, :], op=ALU.add)
            nc.vector.tensor_reduce(out=m[:, 0, 0:n], in_=s[:, 0:n, :], axis=AX.X, op=ALU.max)
            nc.vector.tensor_tensor(
                out=s[:, 0:n, :], in0=s[:, 0:n, :], in1=m[:, 0, 0:n].unsqueeze(2).to_broadcast([P, n, W]), op=ALU.subtract
            )

        def soft_exp(r0, r1):
            n = r1 - r0
            s, e, m = soft[r0]
            nc.scalar.activation(out=e[:, 0:n, :], in_=s[:, 0:n, :], func=ACT.Exp)

        def soft_norm(r0, r1):
            n = r1 - r0
            s, e, m = soft[r0]
            nc.vector.tensor_reduce(out=m[:, 1, 0:n], in_=e[:, 0:n, :], axis=AX.X, op=ALU.add)
            nc.vector.reciprocal(out=m[:, 1, 0:n], in_=m[:, 1, 0:n])
            nc.vector.tensor_tensor(
                out=out_sb[:, r0:r1, :], in0=e[:, 0:n, :], in1=m[:, 1, 0:n].unsqueeze(2).to_broadcast([P, n, W]), op=ALU.mult
            )
            nc.sync.dma_start(out=out_rows[:, r0:r1, :], in_=out_sb[:, r0:r1, :])

        def band_soft_exp():
            nc.vector.tensor_copy(out=picked[:, :, W : 2 * W], in_=picked[:, :, 0:W])
            nc.vector.tensor_scalar_mul(out=band_s[:], in0=picked[:, :, 0:W], scalar1=turned[:, 0:1])
            for m in range(1, W):
                nc.vector.scalar_tensor_tensor(
                    out=band_s[:],
                    in0=picked[:, :, m : m + W],
                    scalar=turned[:, m : m + 1],
                    in1=band_s[:],
                    op0=ALU.mult,
                    op1=ALU.add,
                )
            by_batch = band_s[:].rearrange("p (b h) j -> p b (h j)", h=2)
            nc.vector.tensor_tensor(
                out=by_batch,
                in0=by_batch,
                in1=edge[:].rearrange("p h j -> p (h j)").unsqueeze(1).to_broadcast([P, BAND_TILES // 2, 2 * W]),
                op=ALU.add,
            )
            nc.vector.tensor_reduce(out=band_m[:, 0, :], in_=band_s[:], axis=AX.X, op=ALU.max)
            nc.vector.tensor_tensor(
                out=band_s[:],
                in0=band_s[:],
                in1=band_m[:, 0, :].unsqueeze(2).to_broadcast([P, BAND_TILES, W]),
                op=ALU.subtract,
            )
            nc.scalar.activation(out=band_e[:], in_=band_s[:], func=ACT.Exp)

        def band_soft_norm():
            half = BAND_TILES // 2
            nc.vector.tensor_reduce(out=band_m[:, 1, :], in_=band_e[:], axis=AX.X, op=ALU.add)
            nc.vector.reciprocal(out=band_m[:, 1, :], in_=band_m[:, 1, :])
            nc.vector.tensor_tensor(
                out=band_p[:, :, 0 : W * half].rearrange("p g (t j) -> p g t j", j=W),
                in0=band_e[:].rearrange("p (g t) j -> p g t j", g=2),
                in1=band_m[:, 1, :].rearrange("p (g t) -> p g t", g=2).unsqueeze(3).to_broadcast([P, 2, half, W]),
                op=ALU.mult,
            )
            bank = ps_short.tile([P, 512], F32, name="bank")
            for g in range(2):
                nc.tensor.transpose(bank[:, g * P : (g + 1) * P], band_p[:, g, :], ident[:])
            nc.scalar.copy(out=band_t[:], in_=bank[:, 0 : 2 * P])

        def band_store():
            half = BAND_TILES // 2
            bank = ps_short.tile([P, 512], F32, name="bank")
            for e in range(2):
                nc.tensor.transpose(bank[:, e * P : (e + 1) * P], band_t[:, e : 2 * P : 2], ident[:])
            nc.scalar.copy(
                out=band_o[:],
                in_=bank[:, 0 : 2 * P]
                .rearrange("p (e c) -> p e c", e=2)[:, :, 0 : W * half]
                .rearrange("p e (t j) -> p t e j", j=W),
            )
            for g in range(2):
                t0 = BAND_FIRST[g] * S
                nc.sync.dma_start(
                    out=out_f[t0 : t0 + half * P, :].rearrange("(t u e) j -> u t (e j)", t=half, e=2),
                    in_=band_o[g * 64 : (g + 1) * 64].rearrange("u t e j -> u t (e j)"),
                )

        def burst(b):
            groups = [b] if b <= (NV - 1) // 4 else []
            if b < PAIRS:
                groups.append(R // 4 + b)
            if b % 2 == 1 and b // 2 < NG // 4:
                groups.append(R // 4 - 1 - b // 2)
            return groups

        nc.sync.dma_start(out=w_sb[:], in_=Wq.rearrange("(c p) d -> p c d", p=P))
        load_x(0)
        load_x(R // 4)
        for g in (0, 1):
            load_keys(g)
        load_band_keys(0)
        for e in burst(1):
            load_x(e)
        for g in (10, 9):
            load_keys(g)
        load_band_keys(1)

        make_identity(nc, ident[:])
        nc.gpsimd.iota(place[:], pattern=[[1, R]], base=0, channel_multiplier=R)
        nc.gpsimd.memset(band01[:], 0.0)
        for j in range(W):
            nc.gpsimd.tensor_tensor(out=band01[:, j : j + P], in0=band01[:, j : j + P], in1=ident[:], op=ALU.add)

        nc.vector.memset(b_rows[:], 0.0)
        with nc.allow_non_contiguous_dma(reason="bias, two neighbouring values to a partition"):
            nc.scalar.dma_start(
                out=b_words[:].rearrange("w (u e) -> w u e", e=2), in_=bq.rearrange("(u w e) -> w u e", u=2, e=2)
            )
        nc.scalar.dma_start(out=b_rows[0:4, :], in_=bq.rearrange("(c p) -> c p", p=P))
        nc.vector.memset(mask[:], 0.0)
        nc.vector.memset(edge[:], 0.0)
        nc.vector.memset(band_p[:], 0.0)
        for t in keys_t:
            nc.vector.memset(t[:, :, 0:NB], 0.0)
            nc.vector.memset(t[:, :, NB + S : 2 * NB + S], 0.0)
        for t in kept:
            nc.vector.memset(t[:, :, BW : BW + 3], 0.0)
        nc.vector.tensor_copy(out=ident_bf[:], in_=ident[:])
        for i in range(W):
            nc.vector.tensor_reduce(out=turned[:, i : i + 1], in_=ident[:, i:P:W], axis=AX.X, op=ALU.add)
        nc.vector.tensor_reduce(out=edge[:, 0, 0:1], in_=ident[:, 0:2], axis=AX.X, op=ALU.add)
        nc.vector.tensor_copy(out=edge[:, 0, 1:2], in_=ident[:, 0:1])
        nc.vector.tensor_copy(out=edge[:, 1, 3:4], in_=ident[:, P - 1 : P])
        nc.vector.tensor_reduce(out=edge[:, 1, 4:5], in_=ident[:, P - 2 : P], axis=AX.X, op=ALU.add)
        nc.vector.tensor_scalar_mul(out=edge[:], in0=edge[:], scalar1=NEG)
        nc.vector.tensor_single_scalar(out=place[:], in_=place[:], scalar=S - 1, op=ALU.bitwise_and)
        nc.vector.tensor_copy(out=place_f[:], in_=place[:])
        for j, op, bound in ((0, ALU.is_lt, 2.0), (1, ALU.is_lt, 1.0), (3, ALU.is_gt, S - 2.0), (4, ALU.is_gt, S - 3.0)):
            nc.vector.tensor_scalar(out=mask[:, :, j], in0=place_f[:], scalar1=bound, scalar2=NEG, op0=op, op1=ALU.mult)

        quantise(pack_four(lambda i: w_sb[:].bitcast(F32)[:, i, :], nc.vector.tensor_copy), w_codes[:], w_scales[:])
        stage_x(0)
        stage_x(R // 4)
        quantise_x(0)
        vector_q(0)
        vector_q(1)
        quantise_x(R // 4)
        bank = ps_short.tile([P, 512], F32, name="bank")
        nc.tensor.transpose(bank[:].bitcast(BF16)[:, 0:P], b_rows[:], ident_bf[:])
        nc.scalar.mul(out=b_part[:], in_=bank[:].bitcast(BF16)[:, 0:4], mul=SCALE)

        for t in range(-2, LAST_STEP + 1):
            b = turn(t, -10, 4, 7)
            if b is not None and b >= 2:
                for e in burst(b):
                    load_x(e)
            pi = turn(t, -8, 4, PAIRS)
            if pi is not None and pi >= 2:
                load_band_keys(pi)
            n = turn(t, -1, 1, len(LATER_KEYS))
            if n is not None:
                load_keys(LATER_KEYS[n])

            if t == HR // 2 + 1:
                nc.scalar.mul(out=c_sb[:], in_=c_ps, mul=SCALE)
                for j in range(W):
                    nc.gpsimd.tensor_tensor(out=c_mask[:, :, j], in0=c_sb[:, j : j + R], in1=mask[:, :, j], op=ALU.add)
            if t == 4 * PAIRS + 2:
                band_soft_exp()
            if t == 4 * PAIRS + 3:
                band_soft_norm()
            if t == 4 * PAIRS + 4:
                band_store()
            for first, r0, r1 in SOFT_CHUNKS:
                for n, stage_of_softmax in enumerate((soft_shift, soft_exp, soft_norm)):
                    if t == first + n:
                        stage_of_softmax(r0, r1)

            b = turn(t, -2, 4, 7)
            if b is not None and b >= 1:
                for e in burst(b):
                    quantise_x(e)

            for n in range(3):
                b = turn(t, n - 6, 4, 7)
                if b is not None and b >= 1 and n < len(burst(b)):
                    stage_x(burst(b)[n])
            i = turn(t, 0, 1, HR // 2)
            if i is not None:
                c_transpose(i)
            for be in range(2):
                pi = turn(t, be - 2, 4, PAIRS)
                if pi is not None:
                    band_keys(pi, be)
            i = turn(t, 1, 1, HR // 2)
            if i is not None:
                c_dot(i)
            for be in range(2):
                pi = turn(t, 2 * be + 2, 4, PAIRS)
                if pi is not None:
                    band_scores(pi, be)
            for be in range(2):
                pi = turn(t, be, 4, PAIRS)
                if pi is not None:
                    band_q(pi, 2 * be)
                    band_q(pi, 2 * be + 1)
            m = turn(t, 3, 2, NG)
            if m is not None:
                gpsimd_tile(m)
            if 2 <= t + 2 < NV:
                vector_q(t + 2)

            m = turn(t, 5, 2, NG)
            if m is not None:
                gpsimd_sums(m)

            if 0 <= t < NV:
                vector_tile(t)
            for be in range(2):
                pi = turn(t, 2 * be + 3, 4, PAIRS)
                if pi is not None:
                    band_pick(pi, be)
